import numpy as np
import ml_dtypes


def mxq(x, axis, fmt="e4m3"):
    dtype, down = {"e4m3": (ml_dtypes.float8_e4m3fn, 7), "e5m2": (ml_dtypes.float8_e5m2, 14)}[fmt]
    v = np.moveaxis(np.asarray(x, np.float32).astype(ml_dtypes.bfloat16).astype(np.float64), axis, -1)
    blocks = v.reshape(v.shape[:-1] + (-1, 32))
    amax = np.abs(blocks).max(-1, keepdims=True)
    byte = np.maximum(np.where(amax > 0, np.frexp(amax)[1] - 1 + 127, 0) - down, 1)
    scale = np.exp2(byte - 127.0)
    codes = (blocks / scale).astype(np.float32).astype(dtype).astype(np.float64)
    return np.moveaxis((codes * scale).reshape(v.shape), -1, axis)


WIDE = False


def mx_kscale(k):
    if not WIDE:
        return np.ones(k)
    levels = np.array([10, -10, 5, -5, 0])
    a = np.random.permutation(np.resize(levels, k // 512 * 4)).reshape(k // 512, 4)
    idx = np.arange(k)
    return np.exp2(a[idx // 512, idx % 128 // 32])


BF16 = ml_dtypes.bfloat16


def bf(x):
    return np.asarray(x, np.float32).astype(BF16)


def f64(x):
    return np.asarray(x).astype(np.float64)


E2M1 = np.array([0.0, 0.5, 1.0, 1.5, 2.0, 3.0, 4.0, 6.0, -0.0, -0.5, -1.0, -1.5, -2.0, -3.0, -4.0, -6.0])


def pack_weight(w, fmt):
    k, n = w.shape
    w = f64(bf(w)).reshape(k // 32, 32, n)
    amax = np.abs(w).max(1)
    if fmt == "e4m3":
        byte = np.frexp(amax)[1] - 1 + 127 - 7
    else:
        mant, ex = np.frexp(amax / 6.0)
        byte = np.where(mant > 0.5, ex, ex - 1) + 127
    byte = np.clip(np.where(amax > 0, byte, 1), 1, 254)
    scaled = (w * np.exp2(127.0 - byte)[:, None, :]).reshape(k, n).astype(np.float32)
    by_word = np.ascontiguousarray(scaled.reshape(k // 512, 128, 4, n).transpose(0, 1, 3, 2))
    if fmt == "e4m3":
        words = by_word.astype(ml_dtypes.float8_e4m3fn).view(np.uint8)
    else:
        c = by_word.astype(ml_dtypes.float4_e2m1fn).view(np.uint8) & 0xF
        words = c[..., 0::2] | (c[..., 1::2] << 4)
    return np.ascontiguousarray(words), np.ascontiguousarray(byte.astype(np.uint8).reshape(k // 512, 16, n))


def unpack_weight(words, scales, fmt):
    g, p, n, _ = words.shape
    if fmt == "e4m3":
        vals = np.ascontiguousarray(words).view(ml_dtypes.float8_e4m3fn).astype(np.float64)
    else:
        nib = np.empty((g, p, n, 4), np.uint8)
        nib[..., 0::2] = words & 0xF
        nib[..., 1::2] = words >> 4
        vals = E2M1[nib]
    vals = vals * np.repeat(np.exp2(scales.astype(np.float64) - 127.0), 8, axis=1)[..., None]
    return vals.transpose(0, 1, 3, 2).reshape(g * 512, n)


N, D, C = 2048, 512, 1024


def gaussian_kernel(inputs, centers, gamma):
    x2 = np.sum(inputs * inputs, axis=-1, keepdims=True)
    c2 = np.sum(centers * centers, axis=-1)
    xc = mxq(inputs, 1, "e4m3") @ mxq(centers, 1, "e4m3").T
    sq_dist = np.maximum(x2 + c2[None, :] - 2.0 * xc, 0.0)
    return np.exp(-gamma * sq_dist)


def setup_inputs():
    t = mx_kscale(C)
    gamma = bf((1.0 + 0.1 * np.random.standard_normal(1)) / D)
    g = np.random.standard_normal((C, D))
    shift = np.log(t.max() / t) / f64(gamma)[0]
    centers = g * np.sqrt(1.0 + shift / (g * g).sum(1))[:, None]
    inputs = bf(np.random.standard_normal((N, D)))
    words, scales = pack_weight(np.random.standard_normal((C, C)) * 4.0 / np.sqrt(C) * (t.max() / t)[:, None], "e4m3")
    return {"inputs": inputs, "centers": bf(centers), "gamma": gamma,
            "normalization_words": words, "normalization_scales": scales}


def reference(inputs, centers, gamma, normalization_words, normalization_scales):
    inputs = f64(inputs)
    inputs = inputs.reshape(inputs.shape[0], -1)
    densities = gaussian_kernel(inputs, f64(centers), f64(gamma))
    return mxq(densities, 1, "e4m3") @ unpack_weight(normalization_words, normalization_scales, "e4m3")

@@ -1,0 +1,195 @@
+from contextlib import ExitStack
+
+import concourse.mybir as mybir
+from concourse.masks import make_identity
+
+F32 = mybir.dt.float32
+BF16 = mybir.dt.bfloat16
+I32 = mybir.dt.int32
+U32 = mybir.dt.uint32
+U8 = mybir.dt.uint8
+FP8X4 = mybir.dt.float8_e4m3fn_x4
+ALU = mybir.AluOpType
+ACT = mybir.ActivationFunctionType
+
+P = 128
+PACK = 4
+K_PASS = P * PACK
+BANK = 512
+
+TOKENS, FEATURES, CENTRES = 2048, 512, 1024
+CHUNK = 512
+CHUNKS = TOKENS // CHUNK
+TILES = CHUNK // P
+GROUPS = CENTRES // K_PASS
+HALVES = CENTRES // BANK
+WORDS = FEATURES // 2
+
+FLOPS = 2 * TOKENS * CENTRES * (FEATURES + CENTRES)
+
+
+def quantise_along_features(nc, work, psum_prep, identity, rows, codes, scales):
+    grouped = work.tile([P, 4 * P, PACK], BF16, align_bytes=64)
+    grouped_flat = grouped[:].rearrange("p r t -> p (r t)")
+    grouped_words = grouped_flat.bitcast(F32).rearrange("p (r u) -> p r u", u=2)
+    for pair in range(2):
+        flipped = psum_prep.tile([P, 2, 2 * P], F32, tag="prep")
+        for s in range(2):
+            row_words = rows[:, 2 * pair + s, :].bitcast(F32)
+            for u in range(2):
+                nc.tensor.transpose(
+                    flipped[:, u, s * P : (s + 1) * P], row_words[:, u:WORDS:2], identity
+                )
+        nc.vector.tensor_copy(
+            out=grouped_words[:, pair * 2 * P : (pair + 1) * 2 * P, :],
+            in_=flipped[:].rearrange("p u r -> p r u"),
+        )
+    nc.vector.quantize_mx(out=codes.bitcast(FP8X4), scales=scales, in_=grouped_flat)
+
+
+def sum_of_squares(nc, work, row_tile, total):
+    squares = work.tile([P, FEATURES], BF16)
+    nc.scalar.activation(out=squares[:], in_=row_tile, func=ACT.Square, accum_out=total)
+
+
+def tile_nystroem_kernel(
+    tc, inputs, centers, gamma, normalization_words, normalization_scales, out
+):
+    nc = tc.nc
+    with ExitStack() as ctx:
+        keep = ctx.enter_context(tc.tile_pool(name="keep", bufs=1))
+        work = ctx.enter_context(tc.tile_pool(name="work", bufs=2))
+        results = ctx.enter_context(tc.tile_pool(name="results", bufs=4))
+        psum_prep = ctx.enter_context(tc.psum_pool(name="psum_prep", bufs=2))
+        psum_xc = ctx.enter_context(tc.psum_pool(name="psum_xc", bufs=3))
+        psum_out = ctx.enter_context(tc.psum_pool(name="psum_out", bufs=3))
+
+        x_view = inputs.rearrange("(j p i) d -> j p i d", p=P, i=TILES)
+        c_view = centers.rearrange("(g p t) d -> g p t d", p=P, t=PACK)
+        out_view = out.rearrange("(j p i) n -> j p i n", p=P, i=TILES)
+
+        x_rows = keep.tile([P, CHUNKS, TILES, FEATURES], BF16)
+        c_rows = keep.tile([P, GROUPS, PACK, FEATURES], BF16)
+        gamma_bf16 = keep.tile([P, 1], BF16)
+        w_codes = keep.tile([P, GROUPS, CENTRES], U32, align_bytes=64)
+        w_scales = keep.tile([P, GROUPS, CENTRES], U8, align_bytes=64)
+
+        nc.vector.memset(w_scales[:].bitcast(I32), 0)
+
+        nc.sync.dma_start(out=c_rows[:, 0], in_=c_view[0])
+        nc.sync.dma_start(out=x_rows[:, 0], in_=x_view[0])
+        nc.sync.dma_start(out=c_rows[:, 1], in_=c_view[1])
+        nc.sync.dma_start(out=gamma_bf16[:], in_=gamma.partition_broadcast(P))
+        scale_rows = normalization_scales.bitcast(I32)
+        for quadrant in range(4):
+            nc.sync.dma_start(
+                out=w_scales[32 * quadrant : 32 * quadrant + 4].bitcast(I32),
+                in_=scale_rows[:, 4 * quadrant : 4 * quadrant + 4, :].rearrange("g r n -> r g n"),
+            )
+        word_rows = normalization_words.rearrange("g p n t -> g p (n t)").bitcast(I32)
+        for g in range(GROUPS):
+            nc.sync.dma_start(out=w_codes[:, g, :].bitcast(I32), in_=word_rows[g])
+        for j in range(1, CHUNKS):
+            nc.sync.dma_start(out=x_rows[:, j], in_=x_view[j])
+
+        identity = keep.tile([P, P], F32)
+        make_identity(nc, identity[:])
+        minus_two_gamma = keep.tile([P, 1], F32)
+        nc.vector.tensor_scalar_mul(out=minus_two_gamma[:], in0=gamma_bf16[:], scalar1=-2.0)
+
+        c_codes = keep.tile([P, CENTRES], U32, align_bytes=64)
+        c_scales = keep.tile([P, CENTRES], U8, align_bytes=64)
+        c2 = keep.tile([P, GROUPS * PACK], F32)
+        half_c2 = keep.tile([P, GROUPS * PACK], F32)
+        for g in range(GROUPS):
+            columns = slice(g * K_PASS, (g + 1) * K_PASS)
+            quantise_along_features(
+                nc, work, psum_prep, identity[:], c_rows[:, g], c_codes[:, columns], c_scales[:, columns]
+            )
+            for t in range(PACK):
+                sum_of_squares(nc, work, c_rows[:, g, t, :], c2[:, g * PACK + t : g * PACK + t + 1])
+            nc.vector.tensor_scalar_mul(
+                out=half_c2[:, g * PACK : (g + 1) * PACK],
+                in0=c2[:, g * PACK : (g + 1) * PACK],
+                scalar1=0.5,
+            )
+
+        for j in range(CHUNKS):
+            x_codes = work.tile([P, CHUNK], U32, align_bytes=64)
+            x_scales = work.tile([P, CHUNK], U8, align_bytes=64)
+            quantise_along_features(
+                nc, work, psum_prep, identity[:], x_rows[:, j], x_codes[:], x_scales[:]
+            )
+            x2 = work.tile([P, TILES], F32)
+            for i in range(TILES):
+                sum_of_squares(nc, work, x_rows[:, j, i, :], x2[:, i : i + 1])
+            spread = psum_prep.tile([P, CHUNK], F32, tag="prep")
+            for i in range(TILES):
+                nc.tensor.matmul(
+                    out=spread[:, i * P : (i + 1) * P],
+                    lhsT=x2[:, i : i + 1].to_broadcast([P, P]),
+                    rhs=identity[:],
+                    start=True,
+                    stop=True,
+                )
+            half_x2 = work.tile([P, CHUNK], F32)
+            nc.scalar.mul(out=half_x2[:], in_=spread[:], mul=0.5)
+
+            d_codes = work.tile([P, GROUPS, CHUNK], U32, align_bytes=64)
+            d_scales = work.tile([P, GROUPS, CHUNK], U8, align_bytes=64)
+            for g in range(GROUPS):
+                half_sq = work.tile([P, PACK, CHUNK], F32)
+                for t in range(PACK):
+                    tile_index = g * PACK + t
+                    columns = slice(tile_index * P, (tile_index + 1) * P)
+                    xc = psum_xc.tile([P, CHUNK], F32)
+                    nc.tensor.matmul_mx(
+                        out=xc[:],
+                        lhsT=c_codes[:, columns].bitcast(FP8X4),
+                        lhsT_scale=c_scales[:, columns],
+                        rhs=x_codes[:].bitcast(FP8X4),
+                        rhs_scale=x_scales[:],
+                        start=True,
+                        stop=True,
+                    )
+                    nc.vector.scalar_tensor_tensor(
+                        out=half_sq[:, t, :],
+                        in0=half_x2[:],
+                        scalar=half_c2[:, tile_index : tile_index + 1],
+                        in1=xc[:],
+                        op0=ALU.add,
+                        op1=ALU.subtract,
+                    )
+                clipped = work.tile([P, CHUNK, PACK], F32)
+                nc.vector.tensor_scalar_max(
+                    out=clipped[:], in0=half_sq[:].rearrange("p t w -> p w t"), scalar1=0.0
+                )
+                densities = work.tile([P, CHUNK * PACK], BF16, align_bytes=64)
+                nc.scalar.activation(
+                    out=densities[:],
+                    in_=clipped[:].rearrange("p w t -> p (w t)"),
+                    func=ACT.Exp,
+                    scale=minus_two_gamma[:, 0:1],
+                )
+                nc.vector.quantize_mx(
+                    out=d_codes[:, g, :].bitcast(FP8X4), scales=d_scales[:, g, :], in_=densities[:]
+                )
+
+            for i in range(TILES):
+                tokens = slice(i * P, (i + 1) * P)
+                result = results.tile([P, CENTRES], F32)
+                for h in range(HALVES):
+                    columns = slice(h * BANK, (h + 1) * BANK)
+                    acc = psum_out.tile([P, BANK], F32)
+                    for g in range(GROUPS):
+                        nc.tensor.matmul_mx(
+                            out=acc[:],
+                            lhsT=d_codes[:, g, tokens].bitcast(FP8X4),
+                            lhsT_scale=d_scales[:, g, tokens],
+                            rhs=w_codes[:, g, columns].bitcast(FP8X4),
+                            rhs_scale=w_scales[:, g, columns],
+                            start=(g == 0),
+                            stop=(g == GROUPS - 1),
+                        )
+                    nc.scalar.copy(out=result[:, columns], in_=acc[:])
+                nc.sync.dma_start(out=out_view[j][:, i, :], in_=result[:])

@@ -18,38 +18,21 @@ K_PASS = P * PACK
 BANK = 512
 
 TOKENS, FEATURES, CENTRES = 2048, 512, 1024
-CHUNK = 512
+CHUNK = 256
 CHUNKS = TOKENS // CHUNK
 TILES = CHUNK // P
 GROUPS = CENTRES // K_PASS
+CENTRE_TILES = CENTRES // P
 HALVES = CENTRES // BANK
+OUT_BANKS = TILES * HALVES
 WORDS = FEATURES // 2
 
+EXP_LAG = 1
+QUANTISE_LAG = 2
+FEATURE_LAG = 3
+LARGEST_FLOAT32 = 3.4028234663852886e38
+
 FLOPS = 2 * TOKENS * CENTRES * (FEATURES + CENTRES)
-
-
-def quantise_along_features(nc, work, psum_prep, identity, rows, codes, scales):
-    grouped = work.tile([P, 4 * P, PACK], BF16, align_bytes=64)
-    grouped_flat = grouped[:].rearrange("p r t -> p (r t)")
-    grouped_words = grouped_flat.bitcast(F32).rearrange("p (r u) -> p r u", u=2)
-    for pair in range(2):
-        flipped = psum_prep.tile([P, 2, 2 * P], F32, tag="prep")
-        for s in range(2):
-            row_words = rows[:, 2 * pair + s, :].bitcast(F32)
-            for u in range(2):
-                nc.tensor.transpose(
-                    flipped[:, u, s * P : (s + 1) * P], row_words[:, u:WORDS:2], identity
-                )
-        nc.vector.tensor_copy(
-            out=grouped_words[:, pair * 2 * P : (pair + 1) * 2 * P, :],
-            in_=flipped[:].rearrange("p u r -> p r u"),
-        )
-    nc.vector.quantize_mx(out=codes.bitcast(FP8X4), scales=scales, in_=grouped_flat)
-
-
-def sum_of_squares(nc, work, row_tile, total):
-    squares = work.tile([P, FEATURES], BF16)
-    nc.scalar.activation(out=squares[:], in_=row_tile, func=ACT.Square, accum_out=total)
 
 
 def tile_nystroem_kernel(
@@ -59,10 +42,12 @@ def tile_nystroem_kernel(
     with ExitStack() as ctx:
         keep = ctx.enter_context(tc.tile_pool(name="keep", bufs=1))
         work = ctx.enter_context(tc.tile_pool(name="work", bufs=2))
+        deep = ctx.enter_context(tc.tile_pool(name="deep", bufs=3))
         results = ctx.enter_context(tc.tile_pool(name="results", bufs=4))
         psum_prep = ctx.enter_context(tc.psum_pool(name="psum_prep", bufs=2))
         psum_xc = ctx.enter_context(tc.psum_pool(name="psum_xc", bufs=3))
         psum_out = ctx.enter_context(tc.psum_pool(name="psum_out", bufs=3))
+        ctx.enter_context(tc.manual_schedule())
 
         x_view = inputs.rearrange("(j p i) d -> j p i d", p=P, i=TILES)
         c_view = centers.rearrange("(g p t) d -> g p t d", p=P, t=PACK)
@@ -76,10 +61,12 @@ def tile_nystroem_kernel(
 
         nc.vector.memset(w_scales[:].bitcast(I32), 0)
 
-        nc.sync.dma_start(out=c_rows[:, 0], in_=c_view[0])
         nc.sync.dma_start(out=x_rows[:, 0], in_=x_view[0])
-        nc.sync.dma_start(out=c_rows[:, 1], in_=c_view[1])
+        for g in range(GROUPS):
+            nc.sync.dma_start(out=c_rows[:, g], in_=c_view[g])
         nc.sync.dma_start(out=gamma_bf16[:], in_=gamma.partition_broadcast(P))
+        for j in range(1, FEATURE_LAG):
+            nc.sync.dma_start(out=x_rows[:, j], in_=x_view[j])
         scale_rows = normalization_scales.bitcast(I32)
         for quadrant in range(4):
             nc.sync.dma_start(
@@ -89,107 +76,190 @@ def tile_nystroem_kernel(
         word_rows = normalization_words.rearrange("g p n t -> g p (n t)").bitcast(I32)
         for g in range(GROUPS):
             nc.sync.dma_start(out=w_codes[:, g, :].bitcast(I32), in_=word_rows[g])
-        for j in range(1, CHUNKS):
+        for j in range(FEATURE_LAG, CHUNKS):
             nc.sync.dma_start(out=x_rows[:, j], in_=x_view[j])
 
         identity = keep.tile([P, P], F32)
         make_identity(nc, identity[:])
+        zero = keep.tile([P, 1], F32)
+        one = keep.tile([P, 1], F32)
+        nc.vector.memset(zero[:], 0.0)
+        nc.scalar.activation(out=one[:], in_=zero[:], func=ACT.Exp)
         minus_two_gamma = keep.tile([P, 1], F32)
-        nc.vector.tensor_scalar_mul(out=minus_two_gamma[:], in0=gamma_bf16[:], scalar1=-2.0)
 
         c_codes = keep.tile([P, CENTRES], U32, align_bytes=64)
         c_scales = keep.tile([P, CENTRES], U8, align_bytes=64)
-        c2 = keep.tile([P, GROUPS * PACK], F32)
-        half_c2 = keep.tile([P, GROUPS * PACK], F32)
-        for g in range(GROUPS):
-            columns = slice(g * K_PASS, (g + 1) * K_PASS)
-            quantise_along_features(
-                nc, work, psum_prep, identity[:], c_rows[:, g], c_codes[:, columns], c_scales[:, columns]
+        c2 = keep.tile([P, CENTRE_TILES], F32)
+        half_c2 = keep.tile([P, CENTRE_TILES], F32)
+
+        grouped_x, x_codes, x_scales, x2, half_x2 = {}, {}, {}, {}, {}
+        half_sq, clipped, densities, d_codes, d_scales, result = {}, {}, {}, {}, {}, {}
+
+        def transpose_rows(row_tiles, grouped_columns):
+            grouped_words = (
+                grouped_columns.rearrange("p r t -> p (r t)").bitcast(F32).rearrange("p (r u) -> p r u", u=2)
             )
+            flipped = psum_prep.tile([P, 2, 2 * P], F32, tag="prep")
+            for s in range(2):
+                row_words = row_tiles[:, s, :].bitcast(F32)
+                for u in range(2):
+                    nc.tensor.transpose(
+                        flipped[:, u, s * P : (s + 1) * P], row_words[:, u:WORDS:2], identity[:]
+                    )
+            nc.vector.tensor_copy(out=grouped_words, in_=flipped[:].rearrange("p u r -> p r u"))
+
+        def sum_of_squares(row_tile, total):
+            squares = work.tile([P, FEATURES], BF16)
+            nc.scalar.activation(out=squares[:], in_=row_tile, func=ACT.Square, accum_out=total)
+
+        def centre_squares(g):
+            tiles = slice(g * PACK, (g + 1) * PACK)
             for t in range(PACK):
-                sum_of_squares(nc, work, c_rows[:, g, t, :], c2[:, g * PACK + t : g * PACK + t + 1])
-            nc.vector.tensor_scalar_mul(
-                out=half_c2[:, g * PACK : (g + 1) * PACK],
-                in0=c2[:, g * PACK : (g + 1) * PACK],
-                scalar1=0.5,
+                sum_of_squares(c_rows[:, g, t, :], c2[:, g * PACK + t : g * PACK + t + 1])
+            nc.scalar.mul(out=half_c2[:, tiles], in_=c2[:, tiles], mul=0.5)
+
+        def centre_codes(g):
+            columns = slice(g * K_PASS, (g + 1) * K_PASS)
+            grouped_c = work.tile([P, K_PASS, PACK], BF16, align_bytes=64)
+            for pair in range(PACK // 2):
+                transpose_rows(
+                    c_rows[:, g, 2 * pair : 2 * pair + 2, :], grouped_c[:, pair * 2 * P : (pair + 1) * 2 * P, :]
+                )
+            nc.vector.quantize_mx(
+                out=c_codes[:, columns].bitcast(FP8X4),
+                scales=c_scales[:, columns],
+                in_=grouped_c[:].rearrange("p r t -> p (r t)"),
             )
 
-        for j in range(CHUNKS):
-            x_codes = work.tile([P, CHUNK], U32, align_bytes=64)
-            x_scales = work.tile([P, CHUNK], U8, align_bytes=64)
-            quantise_along_features(
-                nc, work, psum_prep, identity[:], x_rows[:, j], x_codes[:], x_scales[:]
-            )
-            x2 = work.tile([P, TILES], F32)
+        def token_squares(j):
+            x2[j] = work.tile([P, TILES], F32, name="x2")
             for i in range(TILES):
-                sum_of_squares(nc, work, x_rows[:, j, i, :], x2[:, i : i + 1])
+                sum_of_squares(x_rows[:, j, i, :], x2[j][:, i : i + 1])
+
+        def token_codes(j):
+            grouped_x[j] = work.tile([P, CHUNK, PACK], BF16, align_bytes=64, name="grouped_x")
+            transpose_rows(x_rows[:, j], grouped_x[j][:])
+            x_codes[j] = work.tile([P, CHUNK], U32, align_bytes=64, name="x_codes")
+            x_scales[j] = work.tile([P, CHUNK], U8, align_bytes=64, name="x_scales")
+            nc.vector.quantize_mx(
+                out=x_codes[j][:].bitcast(FP8X4),
+                scales=x_scales[j][:],
+                in_=grouped_x[j][:].rearrange("p r t -> p (r t)"),
+            )
             spread = psum_prep.tile([P, CHUNK], F32, tag="prep")
             for i in range(TILES):
                 nc.tensor.matmul(
                     out=spread[:, i * P : (i + 1) * P],
-                    lhsT=x2[:, i : i + 1].to_broadcast([P, P]),
+                    lhsT=x2[j][:, i : i + 1].to_broadcast([P, P]),
                     rhs=identity[:],
                     start=True,
                     stop=True,
                 )
-            half_x2 = work.tile([P, CHUNK], F32)
-            nc.scalar.mul(out=half_x2[:], in_=spread[:], mul=0.5)
+            half_x2[j] = work.tile([P, CHUNK], F32, name="half_x2")
+            nc.vector.tensor_scalar_mul(out=half_x2[j][:], in0=spread[:], scalar1=0.5)
 
-            d_codes = work.tile([P, GROUPS, CHUNK], U32, align_bytes=64)
-            d_scales = work.tile([P, GROUPS, CHUNK], U8, align_bytes=64)
+        def half_distances(j, k):
+            g, t = divmod(k, PACK)
+            columns = slice(k * P, (k + 1) * P)
+            xc = psum_xc.tile([P, CHUNK], F32)
+            nc.tensor.matmul_mx(
+                out=xc[:],
+                lhsT=c_codes[:, columns].bitcast(FP8X4),
+                lhsT_scale=c_scales[:, columns],
+                rhs=x_codes[j][:].bitcast(FP8X4),
+                rhs_scale=x_scales[j][:],
+                start=True,
+                stop=True,
+            )
+            nc.vector.scalar_tensor_tensor(
+                out=half_sq[j][:, g, t, :],
+                in0=half_x2[j][:],
+                scalar=half_c2[:, k : k + 1],
+                in1=xc[:],
+                op0=ALU.add,
+                op1=ALU.subtract,
+            )
+
+        def clip(j):
+            clipped[j] = deep.tile([P, GROUPS, CHUNK, PACK], F32, name="clipped")
+            nc.gpsimd.tensor_scalar(
+                out=clipped[j][:],
+                in0=half_sq[j][:].rearrange("p g t w -> p g w t"),
+                scalar1=LARGEST_FLOAT32,
+                scalar2=0.0,
+                op0=ALU.min,
+                op1=ALU.max,
+            )
+
+        def exponentials(j):
+            densities[j] = deep.tile([P, GROUPS * CHUNK * PACK], BF16, align_bytes=64, name="densities")
+            nc.scalar.activation(
+                out=densities[j][:],
+                in_=clipped[j][:].rearrange("p g w t -> p (g w t)"),
+                func=ACT.Exp,
+                scale=minus_two_gamma[:, 0:1],
+            )
+
+        def quantise_densities(j):
+            d_codes[j] = deep.tile([P, GROUPS * CHUNK], U32, align_bytes=64, name="d_codes")
+            d_scales[j] = deep.tile([P, GROUPS * CHUNK], U8, align_bytes=64, name="d_scales")
+            nc.vector.quantize_mx(
+                out=d_codes[j][:].bitcast(FP8X4), scales=d_scales[j][:], in_=densities[j][:]
+            )
+
+        def feature_matmuls(j, bank):
+            i, h = divmod(bank, HALVES)
+            columns = slice(h * BANK, (h + 1) * BANK)
+            acc = psum_out.tile([P, BANK], F32)
             for g in range(GROUPS):
-                half_sq = work.tile([P, PACK, CHUNK], F32)
-                for t in range(PACK):
-                    tile_index = g * PACK + t
-                    columns = slice(tile_index * P, (tile_index + 1) * P)
-                    xc = psum_xc.tile([P, CHUNK], F32)
-                    nc.tensor.matmul_mx(
-                        out=xc[:],
-                        lhsT=c_codes[:, columns].bitcast(FP8X4),
-                        lhsT_scale=c_scales[:, columns],
-                        rhs=x_codes[:].bitcast(FP8X4),
-                        rhs_scale=x_scales[:],
-                        start=True,
-                        stop=True,
-                    )
-                    nc.vector.scalar_tensor_tensor(
-                        out=half_sq[:, t, :],
-                        in0=half_x2[:],
-                        scalar=half_c2[:, tile_index : tile_index + 1],
-                        in1=xc[:],
-                        op0=ALU.add,
-                        op1=ALU.subtract,
-                    )
-                clipped = work.tile([P, CHUNK, PACK], F32)
-                nc.vector.tensor_scalar_max(
-                    out=clipped[:], in0=half_sq[:].rearrange("p t w -> p w t"), scalar1=0.0
+                tokens = slice(g * CHUNK + i * P, g * CHUNK + (i + 1) * P)
+                nc.tensor.matmul_mx(
+                    out=acc[:],
+                    lhsT=d_codes[j][:, tokens].bitcast(FP8X4),
+                    lhsT_scale=d_scales[j][:, tokens],
+                    rhs=w_codes[:, g, columns].bitcast(FP8X4),
+                    rhs_scale=w_scales[:, g, columns],
+                    start=(g == 0),
+                    stop=(g == GROUPS - 1),
                 )
-                densities = work.tile([P, CHUNK * PACK], BF16, align_bytes=64)
-                nc.scalar.activation(
-                    out=densities[:],
-                    in_=clipped[:].rearrange("p w t -> p (w t)"),
-                    func=ACT.Exp,
-                    scale=minus_two_gamma[:, 0:1],
-                )
-                nc.vector.quantize_mx(
-                    out=d_codes[:, g, :].bitcast(FP8X4), scales=d_scales[:, g, :], in_=densities[:]
-                )
+            return acc
 
-            for i in range(TILES):
-                tokens = slice(i * P, (i + 1) * P)
-                result = results.tile([P, CENTRES], F32)
-                for h in range(HALVES):
-                    columns = slice(h * BANK, (h + 1) * BANK)
-                    acc = psum_out.tile([P, BANK], F32)
-                    for g in range(GROUPS):
-                        nc.tensor.matmul_mx(
-                            out=acc[:],
-                            lhsT=d_codes[:, g, tokens].bitcast(FP8X4),
-                            lhsT_scale=d_scales[:, g, tokens],
-                            rhs=w_codes[:, g, columns].bitcast(FP8X4),
-                            rhs_scale=w_scales[:, g, columns],
-                            start=(g == 0),
-                            stop=(g == GROUPS - 1),
-                        )
-                    nc.scalar.copy(out=result[:, columns], in_=acc[:])
-                nc.sync.dma_start(out=out_view[j][:, i, :], in_=result[:])
+        def empty_bank(copy, j, bank, acc):
+            i, h = divmod(bank, HALVES)
+            if h == 0:
+                result[j] = results.tile([P, CENTRES], F32, name="result")
+            copy(out=result[j][:, h * BANK : (h + 1) * BANK], in_=acc[:])
+            if h == HALVES - 1:
+                nc.sync.dma_start(out=out_view[j][:, i, :], in_=result[j][:])
+
+        token_squares(0)
+        centre_squares(0)
+        centre_squares(1)
+        token_codes(0)
+        for g in range(GROUPS):
+            centre_codes(g)
+        nc.vector.tensor_scalar_mul(out=minus_two_gamma[:], in0=gamma_bf16[:], scalar1=-2.0)
+
+        for s in range(CHUNKS + FEATURE_LAG):
+            if s + 1 < CHUNKS:
+                token_squares(s + 1)
+            if s < CHUNKS:
+                half_sq[s] = work.tile([P, GROUPS, PACK, CHUNK], F32, name="half_sq")
+            for bank in range(OUT_BANKS):
+                if s < CHUNKS:
+                    for k in range(bank * CENTRE_TILES // OUT_BANKS, (bank + 1) * CENTRE_TILES // OUT_BANKS):
+                        half_distances(s, k)
+                if 0 <= s - FEATURE_LAG:
+                    acc = feature_matmuls(s - FEATURE_LAG, bank)
+                    if bank < OUT_BANKS - 1:
+                        empty_bank(nc.scalar.copy, s - FEATURE_LAG, bank, acc)
+            if 0 <= s - EXP_LAG < CHUNKS:
+                exponentials(s - EXP_LAG)
+            if s < CHUNKS:
+                clip(s)
+            if 0 <= s - QUANTISE_LAG < CHUNKS:
+                quantise_densities(s - QUANTISE_LAG)
+            if s + 1 < CHUNKS:
+                token_codes(s + 1)
+            if 0 <= s - FEATURE_LAG:
+                empty_bank(nc.vector.tensor_copy, s - FEATURE_LAG, OUT_BANKS - 1, acc)

@@ -18,21 +18,39 @@ K_PASS = P * PACK
 BANK = 512
 
 TOKENS, FEATURES, CENTRES = 2048, 512, 1024
-CHUNK = 256
-CHUNKS = TOKENS // CHUNK
-TILES = CHUNK // P
+CHUNK_WIDTHS = (256, 512, 512, 512, 256)
 GROUPS = CENTRES // K_PASS
-CENTRE_TILES = CENTRES // P
 HALVES = CENTRES // BANK
-OUT_BANKS = TILES * HALVES
 WORDS = FEATURES // 2
 
-EXP_LAG = 1
-QUANTISE_LAG = 2
-FEATURE_LAG = 3
-LARGEST_FLOAT32 = 3.4028234663852886e38
+VECTOR_TAKES_ONE_BANK_IN = 4
 
 FLOPS = 2 * TOKENS * CENTRES * (FEATURES + CENTRES)
+
+
+def quantise_along_features(nc, work, psum_prep, identity, rows, codes, scales):
+    tiles = rows.shape[1]
+    grouped = work.tile([P, tiles * P, PACK], BF16, align_bytes=64)
+    grouped_flat = grouped[:].rearrange("p r t -> p (r t)")
+    grouped_words = grouped_flat.bitcast(F32).rearrange("p (r u) -> p r u", u=2)
+    for pair in range(tiles // 2):
+        flipped = psum_prep.tile([P, 2, 2 * P], F32, tag="prep")
+        for s in range(2):
+            row_words = rows[:, 2 * pair + s, :].bitcast(F32)
+            for u in range(2):
+                nc.tensor.transpose(
+                    flipped[:, u, s * P : (s + 1) * P], row_words[:, u:WORDS:2], identity
+                )
+        nc.vector.tensor_copy(
+            out=grouped_words[:, pair * 2 * P : (pair + 1) * 2 * P, :],
+            in_=flipped[:].rearrange("p u r -> p r u"),
+        )
+    nc.vector.quantize_mx(out=codes.bitcast(FP8X4), scales=scales, in_=grouped_flat)
+
+
+def sum_of_squares(nc, work, row_tile, total):
+    squares = work.tile([P, FEATURES], BF16)
+    nc.scalar.activation(out=squares[:], in_=row_tile, func=ACT.Square, accum_out=total)
 
 
 def tile_nystroem_kernel(
@@ -41,19 +59,27 @@ def tile_nystroem_kernel(
     nc = tc.nc
     with ExitStack() as ctx:
         keep = ctx.enter_context(tc.tile_pool(name="keep", bufs=1))
-        work = ctx.enter_context(tc.tile_pool(name="work", bufs=2))
-        deep = ctx.enter_context(tc.tile_pool(name="deep", bufs=3))
+        work = ctx.enter_context(tc.tile_pool(name="work", bufs=3))
         results = ctx.enter_context(tc.tile_pool(name="results", bufs=4))
         psum_prep = ctx.enter_context(tc.psum_pool(name="psum_prep", bufs=2))
         psum_xc = ctx.enter_context(tc.psum_pool(name="psum_xc", bufs=3))
         psum_out = ctx.enter_context(tc.psum_pool(name="psum_out", bufs=3))
-        ctx.enter_context(tc.manual_schedule())
 
-        x_view = inputs.rearrange("(j p i) d -> j p i d", p=P, i=TILES)
         c_view = centers.rearrange("(g p t) d -> g p t d", p=P, t=PACK)
-        out_view = out.rearrange("(j p i) n -> j p i n", p=P, i=TILES)
+        chunks = range(len(CHUNK_WIDTHS))
+        first_token = [sum(CHUNK_WIDTHS[:j]) for j in chunks]
+        first_tile = [first_token[j] // P for j in chunks]
+        tiles_of = [CHUNK_WIDTHS[j] // P for j in chunks]
 
-        x_rows = keep.tile([P, CHUNKS, TILES, FEATURES], BF16)
+        def chunk_rows(tensor, j):
+            rows = tensor[first_token[j] : first_token[j] + CHUNK_WIDTHS[j], :]
+            return rows.rearrange("(p i) d -> p i d", p=P)
+
+        def load_tokens(j):
+            tiles = slice(first_tile[j], first_tile[j] + tiles_of[j])
+            nc.sync.dma_start(out=x_rows[:, tiles, :], in_=chunk_rows(inputs, j))
+
+        x_rows = keep.tile([P, TOKENS // P, FEATURES], BF16)
         c_rows = keep.tile([P, GROUPS, PACK, FEATURES], BF16)
         gamma_bf16 = keep.tile([P, 1], BF16)
         w_codes = keep.tile([P, GROUPS, CENTRES], U32, align_bytes=64)
@@ -61,12 +87,11 @@ def tile_nystroem_kernel(
 
         nc.vector.memset(w_scales[:].bitcast(I32), 0)
 
-        nc.sync.dma_start(out=x_rows[:, 0], in_=x_view[0])
-        for g in range(GROUPS):
-            nc.sync.dma_start(out=c_rows[:, g], in_=c_view[g])
+        load_tokens(0)
+        nc.sync.dma_start(out=c_rows[:, 0], in_=c_view[0])
         nc.sync.dma_start(out=gamma_bf16[:], in_=gamma.partition_broadcast(P))
-        for j in range(1, FEATURE_LAG):
-            nc.sync.dma_start(out=x_rows[:, j], in_=x_view[j])
+        nc.sync.dma_start(out=c_rows[:, 1], in_=c_view[1])
+        load_tokens(1)
         scale_rows = normalization_scales.bitcast(I32)
         for quadrant in range(4):
             nc.sync.dma_start(
@@ -76,8 +101,8 @@ def tile_nystroem_kernel(
         word_rows = normalization_words.rearrange("g p n t -> g p (n t)").bitcast(I32)
         for g in range(GROUPS):
             nc.sync.dma_start(out=w_codes[:, g, :].bitcast(I32), in_=word_rows[g])
-        for j in range(FEATURE_LAG, CHUNKS):
-            nc.sync.dma_start(out=x_rows[:, j], in_=x_view[j])
+        for j in chunks[2:]:
+            load_tokens(j)
 
         identity = keep.tile([P, P], F32)
         make_identity(nc, identity[:])
@@ -86,180 +111,121 @@ def tile_nystroem_kernel(
         nc.vector.memset(zero[:], 0.0)
         nc.scalar.activation(out=one[:], in_=zero[:], func=ACT.Exp)
         minus_two_gamma = keep.tile([P, 1], F32)
+        nc.vector.tensor_scalar_mul(out=minus_two_gamma[:], in0=gamma_bf16[:], scalar1=-2.0)
 
         c_codes = keep.tile([P, CENTRES], U32, align_bytes=64)
         c_scales = keep.tile([P, CENTRES], U8, align_bytes=64)
-        c2 = keep.tile([P, CENTRE_TILES], F32)
-        half_c2 = keep.tile([P, CENTRE_TILES], F32)
+        c2 = keep.tile([P, GROUPS * PACK], F32)
+        half_c2 = keep.tile([P, GROUPS * PACK], F32)
 
-        grouped_x, x_codes, x_scales, x2, half_x2 = {}, {}, {}, {}, {}
-        half_sq, clipped, densities, d_codes, d_scales, result = {}, {}, {}, {}, {}, {}
-
-        def transpose_rows(row_tiles, grouped_columns):
-            grouped_words = (
-                grouped_columns.rearrange("p r t -> p (r t)").bitcast(F32).rearrange("p (r u) -> p r u", u=2)
+        def prepare_centres(g):
+            columns = slice(g * K_PASS, (g + 1) * K_PASS)
+            quantise_along_features(
+                nc, work, psum_prep, identity[:], c_rows[:, g], c_codes[:, columns], c_scales[:, columns]
             )
-            flipped = psum_prep.tile([P, 2, 2 * P], F32, tag="prep")
-            for s in range(2):
-                row_words = row_tiles[:, s, :].bitcast(F32)
-                for u in range(2):
-                    nc.tensor.transpose(
-                        flipped[:, u, s * P : (s + 1) * P], row_words[:, u:WORDS:2], identity[:]
-                    )
-            nc.vector.tensor_copy(out=grouped_words, in_=flipped[:].rearrange("p u r -> p r u"))
-
-        def sum_of_squares(row_tile, total):
-            squares = work.tile([P, FEATURES], BF16)
-            nc.scalar.activation(out=squares[:], in_=row_tile, func=ACT.Square, accum_out=total)
-
-        def centre_squares(g):
             tiles = slice(g * PACK, (g + 1) * PACK)
             for t in range(PACK):
-                sum_of_squares(c_rows[:, g, t, :], c2[:, g * PACK + t : g * PACK + t + 1])
+                sum_of_squares(nc, work, c_rows[:, g, t, :], c2[:, g * PACK + t : g * PACK + t + 1])
             nc.scalar.mul(out=half_c2[:, tiles], in_=c2[:, tiles], mul=0.5)
 
-        def centre_codes(g):
-            columns = slice(g * K_PASS, (g + 1) * K_PASS)
-            grouped_c = work.tile([P, K_PASS, PACK], BF16, align_bytes=64)
-            for pair in range(PACK // 2):
-                transpose_rows(
-                    c_rows[:, g, 2 * pair : 2 * pair + 2, :], grouped_c[:, pair * 2 * P : (pair + 1) * 2 * P, :]
-                )
-            nc.vector.quantize_mx(
-                out=c_codes[:, columns].bitcast(FP8X4),
-                scales=c_scales[:, columns],
-                in_=grouped_c[:].rearrange("p r t -> p (r t)"),
-            )
-
-        def token_squares(j):
-            x2[j] = work.tile([P, TILES], F32, name="x2")
-            for i in range(TILES):
-                sum_of_squares(x_rows[:, j, i, :], x2[j][:, i : i + 1])
-
-        def token_codes(j):
-            grouped_x[j] = work.tile([P, CHUNK, PACK], BF16, align_bytes=64, name="grouped_x")
-            transpose_rows(x_rows[:, j], grouped_x[j][:])
-            x_codes[j] = work.tile([P, CHUNK], U32, align_bytes=64, name="x_codes")
-            x_scales[j] = work.tile([P, CHUNK], U8, align_bytes=64, name="x_scales")
-            nc.vector.quantize_mx(
-                out=x_codes[j][:].bitcast(FP8X4),
-                scales=x_scales[j][:],
-                in_=grouped_x[j][:].rearrange("p r t -> p (r t)"),
-            )
-            spread = psum_prep.tile([P, CHUNK], F32, tag="prep")
-            for i in range(TILES):
+        def prepare_tokens(j):
+            width, tiles = CHUNK_WIDTHS[j], tiles_of[j]
+            rows = x_rows[:, first_tile[j] : first_tile[j] + tiles, :]
+            x_codes = work.tile([P, width], U32, align_bytes=64)
+            x_scales = work.tile([P, width], U8, align_bytes=64)
+            x2 = work.tile([P, tiles], F32)
+            for i in range(tiles):
+                sum_of_squares(nc, work, rows[:, i, :], x2[:, i : i + 1])
+            quantise_along_features(nc, work, psum_prep, identity[:], rows, x_codes[:], x_scales[:])
+            spread = psum_prep.tile([P, width], F32, tag="prep")
+            for i in range(tiles):
                 nc.tensor.matmul(
                     out=spread[:, i * P : (i + 1) * P],
-                    lhsT=x2[j][:, i : i + 1].to_broadcast([P, P]),
+                    lhsT=x2[:, i : i + 1].to_broadcast([P, P]),
                     rhs=identity[:],
                     start=True,
                     stop=True,
                 )
-            half_x2[j] = work.tile([P, CHUNK], F32, name="half_x2")
-            nc.vector.tensor_scalar_mul(out=half_x2[j][:], in0=spread[:], scalar1=0.5)
+            half_x2 = work.tile([P, width], F32)
+            nc.vector.tensor_scalar_mul(out=half_x2[:], in0=spread[:], scalar1=0.5)
+            return x_codes, x_scales, half_x2
 
-        def half_distances(j, k):
-            g, t = divmod(k, PACK)
-            columns = slice(k * P, (k + 1) * P)
-            xc = psum_xc.tile([P, CHUNK], F32)
-            nc.tensor.matmul_mx(
-                out=xc[:],
-                lhsT=c_codes[:, columns].bitcast(FP8X4),
-                lhsT_scale=c_scales[:, columns],
-                rhs=x_codes[j][:].bitcast(FP8X4),
-                rhs_scale=x_scales[j][:],
-                start=True,
-                stop=True,
-            )
-            nc.vector.scalar_tensor_tensor(
-                out=half_sq[j][:, g, t, :],
-                in0=half_x2[j][:],
-                scalar=half_c2[:, k : k + 1],
-                in1=xc[:],
-                op0=ALU.add,
-                op1=ALU.subtract,
-            )
-
-        def clip(j):
-            clipped[j] = deep.tile([P, GROUPS, CHUNK, PACK], F32, name="clipped")
-            nc.gpsimd.tensor_scalar(
-                out=clipped[j][:],
-                in0=half_sq[j][:].rearrange("p g t w -> p g w t"),
-                scalar1=LARGEST_FLOAT32,
-                scalar2=0.0,
-                op0=ALU.min,
-                op1=ALU.max,
-            )
-
-        def exponentials(j):
-            densities[j] = deep.tile([P, GROUPS * CHUNK * PACK], BF16, align_bytes=64, name="densities")
-            nc.scalar.activation(
-                out=densities[j][:],
-                in_=clipped[j][:].rearrange("p g w t -> p (g w t)"),
-                func=ACT.Exp,
-                scale=minus_two_gamma[:, 0:1],
-            )
-
-        def quantise_densities(j):
-            d_codes[j] = deep.tile([P, GROUPS * CHUNK], U32, align_bytes=64, name="d_codes")
-            d_scales[j] = deep.tile([P, GROUPS * CHUNK], U8, align_bytes=64, name="d_scales")
-            nc.vector.quantize_mx(
-                out=d_codes[j][:].bitcast(FP8X4), scales=d_scales[j][:], in_=densities[j][:]
-            )
-
-        def feature_matmuls(j, bank):
-            i, h = divmod(bank, HALVES)
-            columns = slice(h * BANK, (h + 1) * BANK)
-            acc = psum_out.tile([P, BANK], F32)
+        def quantised_densities(x_codes, x_scales, half_x2):
+            width = x_codes.shape[1]
+            d_codes = work.tile([P, GROUPS, width], U32, align_bytes=64)
+            d_scales = work.tile([P, GROUPS, width], U8, align_bytes=64)
             for g in range(GROUPS):
-                tokens = slice(g * CHUNK + i * P, g * CHUNK + (i + 1) * P)
-                nc.tensor.matmul_mx(
-                    out=acc[:],
-                    lhsT=d_codes[j][:, tokens].bitcast(FP8X4),
-                    lhsT_scale=d_scales[j][:, tokens],
-                    rhs=w_codes[:, g, columns].bitcast(FP8X4),
-                    rhs_scale=w_scales[:, g, columns],
-                    start=(g == 0),
-                    stop=(g == GROUPS - 1),
+                half_sq = work.tile([P, PACK, width], F32)
+                for t in range(PACK):
+                    tile_index = g * PACK + t
+                    columns = slice(tile_index * P, (tile_index + 1) * P)
+                    xc = psum_xc.tile([P, width], F32)
+                    nc.tensor.matmul_mx(
+                        out=xc[:],
+                        lhsT=c_codes[:, columns].bitcast(FP8X4),
+                        lhsT_scale=c_scales[:, columns],
+                        rhs=x_codes[:].bitcast(FP8X4),
+                        rhs_scale=x_scales[:],
+                        start=True,
+                        stop=True,
+                    )
+                    nc.vector.scalar_tensor_tensor(
+                        out=half_sq[:, t, :],
+                        in0=half_x2[:],
+                        scalar=half_c2[:, tile_index : tile_index + 1],
+                        in1=xc[:],
+                        op0=ALU.add,
+                        op1=ALU.subtract,
+                    )
+                exponents = work.tile([P, width, PACK], F32)
+                nc.vector.tensor_scalar(
+                    out=exponents[:],
+                    in0=half_sq[:].rearrange("p t w -> p w t"),
+                    scalar1=0.0,
+                    scalar2=minus_two_gamma[:, 0:1],
+                    op0=ALU.max,
+                    op1=ALU.mult,
                 )
-            return acc
+                densities = work.tile([P, width * PACK], BF16, align_bytes=64)
+                nc.scalar.activation(
+                    out=densities[:],
+                    in_=exponents[:].rearrange("p w t -> p (w t)"),
+                    func=ACT.Exp,
+                )
+                nc.vector.quantize_mx(
+                    out=d_codes[:, g, :].bitcast(FP8X4), scales=d_scales[:, g, :], in_=densities[:]
+                )
+            return d_codes, d_scales
 
-        def empty_bank(copy, j, bank, acc):
-            i, h = divmod(bank, HALVES)
-            if h == 0:
-                result[j] = results.tile([P, CENTRES], F32, name="result")
-            copy(out=result[j][:, h * BANK : (h + 1) * BANK], in_=acc[:])
-            if h == HALVES - 1:
-                nc.sync.dma_start(out=out_view[j][:, i, :], in_=result[j][:])
+        def features(j, d_codes, d_scales):
+            for i in range(tiles_of[j]):
+                tokens = slice(i * P, (i + 1) * P)
+                result = results.tile([P, CENTRES], F32)
+                for h in range(HALVES):
+                    columns = slice(h * BANK, (h + 1) * BANK)
+                    acc = psum_out.tile([P, BANK], F32)
+                    for g in range(GROUPS):
+                        nc.tensor.matmul_mx(
+                            out=acc[:],
+                            lhsT=d_codes[:, g, tokens].bitcast(FP8X4),
+                            lhsT_scale=d_scales[:, g, tokens],
+                            rhs=w_codes[:, g, columns].bitcast(FP8X4),
+                            rhs_scale=w_scales[:, g, columns],
+                            start=(g == 0),
+                            stop=(g == GROUPS - 1),
+                        )
+                    if (i * HALVES + h) % VECTOR_TAKES_ONE_BANK_IN == VECTOR_TAKES_ONE_BANK_IN - 1:
+                        nc.vector.tensor_copy(out=result[:, columns], in_=acc[:])
+                    else:
+                        nc.scalar.copy(out=result[:, columns], in_=acc[:])
+                nc.sync.dma_start(out=chunk_rows(out, j)[:, i, :], in_=result[:])
 
-        token_squares(0)
-        centre_squares(0)
-        centre_squares(1)
-        token_codes(0)
+        prepared = prepare_tokens(0)
         for g in range(GROUPS):
-            centre_codes(g)
-        nc.vector.tensor_scalar_mul(out=minus_two_gamma[:], in0=gamma_bf16[:], scalar1=-2.0)
-
-        for s in range(CHUNKS + FEATURE_LAG):
-            if s + 1 < CHUNKS:
-                token_squares(s + 1)
-            if s < CHUNKS:
-                half_sq[s] = work.tile([P, GROUPS, PACK, CHUNK], F32, name="half_sq")
-            for bank in range(OUT_BANKS):
-                if s < CHUNKS:
-                    for k in range(bank * CENTRE_TILES // OUT_BANKS, (bank + 1) * CENTRE_TILES // OUT_BANKS):
-                        half_distances(s, k)
-                if 0 <= s - FEATURE_LAG:
-                    acc = feature_matmuls(s - FEATURE_LAG, bank)
-                    if bank < OUT_BANKS - 1:
-                        empty_bank(nc.scalar.copy, s - FEATURE_LAG, bank, acc)
-            if 0 <= s - EXP_LAG < CHUNKS:
-                exponentials(s - EXP_LAG)
-            if s < CHUNKS:
-                clip(s)
-            if 0 <= s - QUANTISE_LAG < CHUNKS:
-                quantise_densities(s - QUANTISE_LAG)
-            if s + 1 < CHUNKS:
-                token_codes(s + 1)
-            if 0 <= s - FEATURE_LAG:
-                empty_bank(nc.vector.tensor_copy, s - FEATURE_LAG, OUT_BANKS - 1, acc)
+            prepare_centres(g)
+        for j in chunks:
+            current = prepared
+            if j + 1 < len(CHUNK_WIDTHS):
+                prepared = prepare_tokens(j + 1)
+            d_codes, d_scales = quantised_densities(*current)
+            features(j, d_codes, d_scales)

@@ -23,6 +23,7 @@ GROUPS = CENTRES // K_PASS
 HALVES = CENTRES // BANK
 WORDS = FEATURES // 2
 
+RUN = 4
 VECTOR_TAKES_ONE_BANK_IN = 4
 
 FLOPS = 2 * TOKENS * CENTRES * (FEATURES + CENTRES)
@@ -179,8 +180,8 @@ def tile_nystroem_kernel(
                     )
                 exponents = work.tile([P, width, PACK], F32)
                 nc.vector.tensor_scalar(
-                    out=exponents[:],
-                    in0=half_sq[:].rearrange("p t w -> p w t"),
+                    out=exponents[:].rearrange("p (c i) t -> p c t i", i=RUN),
+                    in0=half_sq[:].rearrange("p t (c i) -> p c t i", i=RUN),
                     scalar1=0.0,
                     scalar2=minus_two_gamma[:, 0:1],
                     op0=ALU.max,

@@ -23,6 +23,7 @@ GROUPS = CENTRES // K_PASS
 HALVES = CENTRES // BANK
 WORDS = FEATURES // 2
 
+UNBOUNDED = 3.0e38
 RUN = 4
 VECTOR_TAKES_ONE_BANK_IN = 4
 
@@ -113,6 +114,14 @@ def tile_nystroem_kernel(
         nc.scalar.activation(out=one[:], in_=zero[:], func=ACT.Exp)
         minus_two_gamma = keep.tile([P, 1], F32)
         nc.vector.tensor_scalar_mul(out=minus_two_gamma[:], in0=gamma_bf16[:], scalar1=-2.0)
+        lowest = keep.tile([P, 1], F32)
+        highest = keep.tile([P, 1], F32)
+        nc.vector.tensor_scalar(
+            out=lowest[:], in0=minus_two_gamma[:], scalar1=0.0, scalar2=None, op0=ALU.is_gt
+        )
+        nc.vector.tensor_scalar(
+            out=highest[:], in0=lowest[:], scalar1=UNBOUNDED, scalar2=1.0, op0=ALU.mult, op1=ALU.add
+        )
 
         c_codes = keep.tile([P, CENTRES], U32, align_bytes=64)
         c_scales = keep.tile([P, CENTRES], U8, align_bytes=64)
@@ -178,20 +187,20 @@ def tile_nystroem_kernel(
                         op0=ALU.add,
                         op1=ALU.subtract,
                     )
-                exponents = work.tile([P, width, PACK], F32)
-                nc.vector.tensor_scalar(
-                    out=exponents[:].rearrange("p (c i) t -> p c t i", i=RUN),
-                    in0=half_sq[:].rearrange("p t (c i) -> p c t i", i=RUN),
-                    scalar1=0.0,
-                    scalar2=minus_two_gamma[:, 0:1],
-                    op0=ALU.max,
-                    op1=ALU.mult,
-                )
                 densities = work.tile([P, width * PACK], BF16, align_bytes=64)
                 nc.scalar.activation(
-                    out=densities[:],
-                    in_=exponents[:].rearrange("p w t -> p (w t)"),
+                    out=densities[:].rearrange("p (c i t) -> p c t i", i=RUN, t=PACK),
+                    in_=half_sq[:].rearrange("p t (c i) -> p c t i", i=RUN),
                     func=ACT.Exp,
+                    scale=minus_two_gamma[:, 0:1],
+                )
+                nc.vector.tensor_scalar(
+                    out=densities[:],
+                    in0=densities[:],
+                    scalar1=highest[:, 0:1],
+                    scalar2=lowest[:, 0:1],
+                    op0=ALU.min,
+                    op1=ALU.max,
                 )
                 nc.vector.quantize_mx(
                     out=d_codes[:, g, :].bitcast(FP8X4), scales=d_scales[:, g, :], in_=densities[:]

@@ -18,36 +18,33 @@ K_PASS = P * PACK
 BANK = 512
 
 TOKENS, FEATURES, CENTRES = 2048, 512, 1024
-CHUNK_WIDTHS = (256, 512, 512, 512, 256)
+CHUNK = 512
+CHUNKS = TOKENS // CHUNK
+TILES = CHUNK // P
 GROUPS = CENTRES // K_PASS
 HALVES = CENTRES // BANK
 WORDS = FEATURES // 2
 
 UNBOUNDED = 3.0e38
 RUN = 4
-VECTOR_TAKES_ONE_BANK_IN = 4
+
+VECTOR_BANKS = (4, 6)
 
 FLOPS = 2 * TOKENS * CENTRES * (FEATURES + CENTRES)
 
 
-def quantise_along_features(nc, work, psum_prep, identity, rows, codes, scales):
-    tiles = rows.shape[1]
-    grouped = work.tile([P, tiles * P, PACK], BF16, align_bytes=64)
-    grouped_flat = grouped[:].rearrange("p r t -> p (r t)")
-    grouped_words = grouped_flat.bitcast(F32).rearrange("p (r u) -> p r u", u=2)
-    for pair in range(tiles // 2):
-        flipped = psum_prep.tile([P, 2, 2 * P], F32, tag="prep")
-        for s in range(2):
-            row_words = rows[:, 2 * pair + s, :].bitcast(F32)
-            for u in range(2):
-                nc.tensor.transpose(
-                    flipped[:, u, s * P : (s + 1) * P], row_words[:, u:WORDS:2], identity
-                )
-        nc.vector.tensor_copy(
-            out=grouped_words[:, pair * 2 * P : (pair + 1) * 2 * P, :],
-            in_=flipped[:].rearrange("p u r -> p r u"),
-        )
-    nc.vector.quantize_mx(out=codes.bitcast(FP8X4), scales=scales, in_=grouped_flat)
+def transpose_pair(nc, psum_side, identity, rows, pair):
+    flipped = psum_side.tile([P, 2, 2 * P], F32, tag="side")
+    for s in range(2):
+        row_words = rows[:, 2 * pair + s, :].bitcast(F32)
+        for u in range(2):
+            nc.tensor.transpose(flipped[:, u, s * P : (s + 1) * P], row_words[:, u:WORDS:2], identity)
+    return flipped
+
+
+def regroup_pair(copy, flipped, grouped, pair):
+    words = grouped.rearrange("p r t -> p (r t)").bitcast(F32).rearrange("p (r u) -> p r u", u=2)
+    copy(out=words[:, pair * 2 * P : (pair + 1) * 2 * P, :], in_=flipped[:].rearrange("p u r -> p r u"))
 
 
 def sum_of_squares(nc, work, row_tile, total):
@@ -62,24 +59,20 @@ def tile_nystroem_kernel(
     with ExitStack() as ctx:
         keep = ctx.enter_context(tc.tile_pool(name="keep", bufs=1))
         work = ctx.enter_context(tc.tile_pool(name="work", bufs=3))
-        results = ctx.enter_context(tc.tile_pool(name="results", bufs=4))
-        psum_prep = ctx.enter_context(tc.psum_pool(name="psum_prep", bufs=2))
-        psum_xc = ctx.enter_context(tc.psum_pool(name="psum_xc", bufs=3))
-        psum_out = ctx.enter_context(tc.psum_pool(name="psum_out", bufs=3))
+        results = ctx.enter_context(tc.tile_pool(name="results", bufs=6))
+        psum_xc = ctx.enter_context(tc.psum_pool(name="psum_xc", bufs=4))
+        psum_side = ctx.enter_context(tc.psum_pool(name="psum_side", bufs=4))
 
         c_view = centers.rearrange("(g p t) d -> g p t d", p=P, t=PACK)
-        chunks = range(len(CHUNK_WIDTHS))
-        first_token = [sum(CHUNK_WIDTHS[:j]) for j in chunks]
-        first_tile = [first_token[j] // P for j in chunks]
-        tiles_of = [CHUNK_WIDTHS[j] // P for j in chunks]
 
         def chunk_rows(tensor, j):
-            rows = tensor[first_token[j] : first_token[j] + CHUNK_WIDTHS[j], :]
-            return rows.rearrange("(p i) d -> p i d", p=P)
+            return tensor[j * CHUNK : (j + 1) * CHUNK, :].rearrange("(p i) d -> p i d", p=P)
+
+        def token_rows(j):
+            return x_rows[:, j * TILES : (j + 1) * TILES, :]
 
         def load_tokens(j):
-            tiles = slice(first_tile[j], first_tile[j] + tiles_of[j])
-            nc.sync.dma_start(out=x_rows[:, tiles, :], in_=chunk_rows(inputs, j))
+            nc.sync.dma_start(out=token_rows(j), in_=chunk_rows(inputs, j))
 
         x_rows = keep.tile([P, TOKENS // P, FEATURES], BF16)
         c_rows = keep.tile([P, GROUPS, PACK, FEATURES], BF16)
@@ -89,9 +82,13 @@ def tile_nystroem_kernel(
 
         nc.vector.memset(w_scales[:].bitcast(I32), 0)
 
-        load_tokens(0)
-        nc.sync.dma_start(out=c_rows[:, 0], in_=c_view[0])
-        nc.sync.dma_start(out=gamma_bf16[:], in_=gamma.partition_broadcast(P))
+        nc.scalar.dma_start(out=gamma_bf16[:], in_=gamma.partition_broadcast(P))
+        for pair in range(TILES // 2):
+            tiles = slice(2 * pair, 2 * pair + 2)
+            nc.sync.dma_start(out=token_rows(0)[:, tiles, :], in_=chunk_rows(inputs, 0)[:, tiles, :])
+        for pair in range(PACK // 2):
+            tiles = slice(2 * pair, 2 * pair + 2)
+            nc.sync.dma_start(out=c_rows[:, 0, tiles, :], in_=c_view[0][:, tiles, :])
         nc.sync.dma_start(out=c_rows[:, 1], in_=c_view[1])
         load_tokens(1)
         scale_rows = normalization_scales.bitcast(I32)
@@ -103,7 +100,7 @@ def tile_nystroem_kernel(
         word_rows = normalization_words.rearrange("g p n t -> g p (n t)").bitcast(I32)
         for g in range(GROUPS):
             nc.sync.dma_start(out=w_codes[:, g, :].bitcast(I32), in_=word_rows[g])
-        for j in chunks[2:]:
+        for j in range(2, CHUNKS):
             load_tokens(j)
 
         identity = keep.tile([P, P], F32)
@@ -113,129 +110,296 @@ def tile_nystroem_kernel(
         nc.vector.memset(zero[:], 0.0)
         nc.scalar.activation(out=one[:], in_=zero[:], func=ACT.Exp)
         minus_two_gamma = keep.tile([P, 1], F32)
-        nc.vector.tensor_scalar_mul(out=minus_two_gamma[:], in0=gamma_bf16[:], scalar1=-2.0)
         lowest = keep.tile([P, 1], F32)
         highest = keep.tile([P, 1], F32)
-        nc.vector.tensor_scalar(
-            out=lowest[:], in0=minus_two_gamma[:], scalar1=0.0, scalar2=None, op0=ALU.is_gt
-        )
-        nc.vector.tensor_scalar(
-            out=highest[:], in0=lowest[:], scalar1=UNBOUNDED, scalar2=1.0, op0=ALU.mult, op1=ALU.add
-        )
+
+        def read_gamma():
+            nc.vector.tensor_scalar_mul(out=minus_two_gamma[:], in0=gamma_bf16[:], scalar1=-2.0)
+            nc.vector.tensor_scalar(
+                out=lowest[:], in0=minus_two_gamma[:], scalar1=0.0, scalar2=None, op0=ALU.is_gt
+            )
+            nc.vector.tensor_scalar(
+                out=highest[:], in0=lowest[:], scalar1=UNBOUNDED, scalar2=1.0, op0=ALU.mult, op1=ALU.add
+            )
 
         c_codes = keep.tile([P, CENTRES], U32, align_bytes=64)
         c_scales = keep.tile([P, CENTRES], U8, align_bytes=64)
         c2 = keep.tile([P, GROUPS * PACK], F32)
         half_c2 = keep.tile([P, GROUPS * PACK], F32)
 
-        def prepare_centres(g):
-            columns = slice(g * K_PASS, (g + 1) * K_PASS)
-            quantise_along_features(
-                nc, work, psum_prep, identity[:], c_rows[:, g], c_codes[:, columns], c_scales[:, columns]
-            )
+        flipped_of = {}
+        grouped_of = {}
+        x2_of = {}
+        spread_of = {}
+        tokens_of = {}
+
+        def centre_squares(g):
             tiles = slice(g * PACK, (g + 1) * PACK)
             for t in range(PACK):
                 sum_of_squares(nc, work, c_rows[:, g, t, :], c2[:, g * PACK + t : g * PACK + t + 1])
             nc.scalar.mul(out=half_c2[:, tiles], in_=c2[:, tiles], mul=0.5)
 
-        def prepare_tokens(j):
-            width, tiles = CHUNK_WIDTHS[j], tiles_of[j]
-            rows = x_rows[:, first_tile[j] : first_tile[j] + tiles, :]
-            x_codes = work.tile([P, width], U32, align_bytes=64)
-            x_scales = work.tile([P, width], U8, align_bytes=64)
-            x2 = work.tile([P, tiles], F32)
-            for i in range(tiles):
-                sum_of_squares(nc, work, rows[:, i, :], x2[:, i : i + 1])
-            quantise_along_features(nc, work, psum_prep, identity[:], rows, x_codes[:], x_scales[:])
-            spread = psum_prep.tile([P, width], F32, tag="prep")
-            for i in range(tiles):
-                nc.tensor.matmul(
-                    out=spread[:, i * P : (i + 1) * P],
-                    lhsT=x2[:, i : i + 1].to_broadcast([P, P]),
-                    rhs=identity[:],
-                    start=True,
-                    stop=True,
-                )
-            half_x2 = work.tile([P, width], F32)
-            nc.vector.tensor_scalar_mul(out=half_x2[:], in0=spread[:], scalar1=0.5)
-            return x_codes, x_scales, half_x2
+        def centre_transposes(g):
+            return [transpose_pair(nc, psum_side, identity[:], c_rows[:, g], pair) for pair in range(PACK // 2)]
 
-        def quantised_densities(x_codes, x_scales, half_x2):
-            width = x_codes.shape[1]
-            d_codes = work.tile([P, GROUPS, width], U32, align_bytes=64)
-            d_scales = work.tile([P, GROUPS, width], U8, align_bytes=64)
-            for g in range(GROUPS):
+        def centre_regroup(flipped, copy):
+            grouped = work.tile([P, K_PASS, PACK], BF16, align_bytes=64)
+            for pair in range(PACK // 2):
+                regroup_pair(copy, flipped[pair], grouped[:], pair)
+            return grouped
+
+        def centre_codes(g, grouped):
+            for pair in range(PACK // 2):
+                first = g * K_PASS + pair * 2 * P
+                columns = slice(first, first + 2 * P)
+                nc.vector.quantize_mx(
+                    out=c_codes[:, columns].bitcast(FP8X4),
+                    scales=c_scales[:, columns],
+                    in_=grouped[:, pair * 2 * P : (pair + 1) * 2 * P, :].rearrange("p r t -> p (r t)"),
+                )
+
+        def token_squares(j):
+            x2 = work.tile([P, TILES], F32)
+            for i in range(TILES):
+                sum_of_squares(nc, work, token_rows(j)[:, i, :], x2[:, i : i + 1])
+            x2_of[j] = x2
+
+        def token_transposes(j, pair):
+            flipped_of[j, pair] = transpose_pair(nc, psum_side, identity[:], token_rows(j), pair)
+
+        def token_regroup(j, pair, copy):
+            if j not in grouped_of:
+                grouped = work.tile([P, CHUNK, PACK], BF16, align_bytes=64)
+                grouped_of[j] = grouped
+            regroup_pair(copy, flipped_of[j, pair], grouped_of[j][:], pair)
+
+        def token_codes(j):
+            x_codes = work.tile([P, CHUNK], U32, align_bytes=64)
+            x_scales = work.tile([P, CHUNK], U8, align_bytes=64)
+            nc.vector.quantize_mx(
+                out=x_codes[:].bitcast(FP8X4), scales=x_scales[:], in_=grouped_of[j][:].rearrange("p r t -> p (r t)")
+            )
+            tokens_of[j] = (x_codes, x_scales)
+
+        def spread_squares(j):
+            spread = psum_side.tile([P, CHUNK], F32, tag="side")
+            for i in range(TILES):
+                nc.tensor.transpose(
+                    spread[:, i * P : (i + 1) * P], x2_of[j][:, i : i + 1].to_broadcast([P, P]), identity[:]
+                )
+            spread_of[j] = spread
+
+        def keep_squares(j):
+            half_x2 = work.tile([P, CHUNK], F32)
+            nc.vector.tensor_scalar_mul(out=half_x2[:], in0=spread_of[j][:], scalar1=0.5)
+            half_x2_of[j] = half_x2
+
+        units = [(j, g, 0, CHUNK) for j in range(CHUNKS - 1) for g in range(GROUPS)]
+        drain = len(units)
+        units += [(CHUNKS - 1, g, first, CHUNK // 2) for first in (0, CHUNK // 2) for g in range(GROUPS)]
+        half_x2_of = {}
+        xc_of = {}
+        half_sq_of = {}
+        density_of = {}
+        d_codes_of = {}
+        bank_of = {}
+        result_of = {}
+
+        def first_matmul(u, t):
+            j, g, start, width = units[u]
+            x_codes, x_scales = tokens_of[j]
+            columns = slice((g * PACK + t) * P, (g * PACK + t + 1) * P)
+            xc = psum_xc.tile([P, width], F32)
+            nc.tensor.matmul_mx(
+                out=xc[:],
+                lhsT=c_codes[:, columns].bitcast(FP8X4),
+                lhsT_scale=c_scales[:, columns],
+                rhs=x_codes[:, start : start + width].bitcast(FP8X4),
+                rhs_scale=x_scales[:, start : start + width],
+                start=True,
+                stop=True,
+            )
+            xc_of[u, t] = xc
+
+        def distance(u, t):
+            j, g, start, width = units[u]
+            if t == 0:
                 half_sq = work.tile([P, PACK, width], F32)
-                for t in range(PACK):
-                    tile_index = g * PACK + t
-                    columns = slice(tile_index * P, (tile_index + 1) * P)
-                    xc = psum_xc.tile([P, width], F32)
-                    nc.tensor.matmul_mx(
-                        out=xc[:],
-                        lhsT=c_codes[:, columns].bitcast(FP8X4),
-                        lhsT_scale=c_scales[:, columns],
-                        rhs=x_codes[:].bitcast(FP8X4),
-                        rhs_scale=x_scales[:],
-                        start=True,
-                        stop=True,
-                    )
-                    nc.vector.scalar_tensor_tensor(
-                        out=half_sq[:, t, :],
-                        in0=half_x2[:],
-                        scalar=half_c2[:, tile_index : tile_index + 1],
-                        in1=xc[:],
-                        op0=ALU.add,
-                        op1=ALU.subtract,
-                    )
-                densities = work.tile([P, width * PACK], BF16, align_bytes=64)
+                half_sq_of[u] = half_sq
+            nc.vector.scalar_tensor_tensor(
+                out=half_sq_of[u][:, t, :],
+                in0=half_x2_of[j][:, start : start + width],
+                scalar=half_c2[:, g * PACK + t : g * PACK + t + 1],
+                in1=xc_of[u, t][:],
+                op0=ALU.add,
+                op1=ALU.subtract,
+            )
+
+        def exponential(u):
+            width = units[u][3]
+            densities = work.tile([P, width * PACK], BF16, align_bytes=64)
+            for first in range(0, width, strip_of(u)):
+                strip = slice(first, first + strip_of(u))
                 nc.scalar.activation(
-                    out=densities[:].rearrange("p (c i t) -> p c t i", i=RUN, t=PACK),
-                    in_=half_sq[:].rearrange("p t (c i) -> p c t i", i=RUN),
+                    out=densities[:, first * PACK : strip.stop * PACK].rearrange(
+                        "p (c i t) -> p c t i", i=RUN, t=PACK
+                    ),
+                    in_=half_sq_of[u][:, :, strip].rearrange("p t (c i) -> p c t i", i=RUN),
                     func=ACT.Exp,
                     scale=minus_two_gamma[:, 0:1],
                 )
-                nc.vector.tensor_scalar(
-                    out=densities[:],
-                    in0=densities[:],
-                    scalar1=highest[:, 0:1],
-                    scalar2=lowest[:, 0:1],
-                    op0=ALU.min,
-                    op1=ALU.max,
-                )
-                nc.vector.quantize_mx(
-                    out=d_codes[:, g, :].bitcast(FP8X4), scales=d_scales[:, g, :], in_=densities[:]
-                )
-            return d_codes, d_scales
+            density_of[u] = densities
 
-        def features(j, d_codes, d_scales):
-            for i in range(tiles_of[j]):
-                tokens = slice(i * P, (i + 1) * P)
+        def strip_of(u):
+            return P if u == len(units) - 1 else units[u][3]
+
+        def strip_values(u, first):
+            return density_of[u][:, first * PACK : (first + strip_of(u)) * PACK]
+
+        def bound(u, first):
+            values = strip_values(u, first)
+            nc.vector.tensor_scalar(
+                out=values, in0=values, scalar1=highest[:, 0:1], scalar2=lowest[:, 0:1], op0=ALU.min, op1=ALU.max
+            )
+
+        def quantise(u, first):
+            j, g, start, width = units[u]
+            if j not in d_codes_of:
+                d_codes = work.tile([P, GROUPS, CHUNK], U32, align_bytes=64)
+                d_scales = work.tile([P, GROUPS, CHUNK], U8, align_bytes=64)
+                d_codes_of[j] = (d_codes, d_scales)
+            d_codes, d_scales = d_codes_of[j]
+            tokens = slice(start + first, start + first + strip_of(u))
+            nc.vector.quantize_mx(
+                out=d_codes[:, g, tokens].bitcast(FP8X4),
+                scales=d_scales[:, g, tokens],
+                in_=strip_values(u, first),
+            )
+
+        def second_matmul(j, b):
+            i, h = divmod(b, HALVES)
+            d_codes, d_scales = d_codes_of[j]
+            tokens = slice(i * P, (i + 1) * P)
+            columns = slice(h * BANK, (h + 1) * BANK)
+            acc = psum_side.tile([P, BANK], F32, tag="side")
+            for g in range(GROUPS):
+                nc.tensor.matmul_mx(
+                    out=acc[:],
+                    lhsT=d_codes[:, g, tokens].bitcast(FP8X4),
+                    lhsT_scale=d_scales[:, g, tokens],
+                    rhs=w_codes[:, g, columns].bitcast(FP8X4),
+                    rhs_scale=w_scales[:, g, columns],
+                    start=(g == 0),
+                    stop=(g == GROUPS - 1),
+                )
+            bank_of[j, b] = acc
+
+        def empty(copy, j, b):
+            i, h = divmod(b, HALVES)
+            if h == 0:
                 result = results.tile([P, CENTRES], F32)
-                for h in range(HALVES):
-                    columns = slice(h * BANK, (h + 1) * BANK)
-                    acc = psum_out.tile([P, BANK], F32)
-                    for g in range(GROUPS):
-                        nc.tensor.matmul_mx(
-                            out=acc[:],
-                            lhsT=d_codes[:, g, tokens].bitcast(FP8X4),
-                            lhsT_scale=d_scales[:, g, tokens],
-                            rhs=w_codes[:, g, columns].bitcast(FP8X4),
-                            rhs_scale=w_scales[:, g, columns],
-                            start=(g == 0),
-                            stop=(g == GROUPS - 1),
-                        )
-                    if (i * HALVES + h) % VECTOR_TAKES_ONE_BANK_IN == VECTOR_TAKES_ONE_BANK_IN - 1:
-                        nc.vector.tensor_copy(out=result[:, columns], in_=acc[:])
-                    else:
-                        nc.scalar.copy(out=result[:, columns], in_=acc[:])
-                nc.sync.dma_start(out=chunk_rows(out, j)[:, i, :], in_=result[:])
+                result_of[j, i] = result
+            copy(out=result_of[j, i][:, h * BANK : (h + 1) * BANK], in_=bank_of[j, b][:])
+            if h == HALVES - 1:
+                nc.sync.dma_start(out=chunk_rows(out, j)[:, i, :], in_=result_of[j, i][:])
 
-        prepared = prepare_tokens(0)
-        for g in range(GROUPS):
-            prepare_centres(g)
-        for j in chunks:
-            current = prepared
-            if j + 1 < len(CHUNK_WIDTHS):
-                prepared = prepare_tokens(j + 1)
-            d_codes, d_scales = quantised_densities(*current)
-            features(j, d_codes, d_scales)
+        by_vector = nc.vector.tensor_copy
+        by_scalar = nc.scalar.copy
+        banks = range(HALVES * TILES)
+        pairs = range(TILES // 2)
+        with tc.manual_schedule():
+            token_squares(0)
+            for pair in pairs:
+                token_transposes(0, pair)
+            flipped = centre_transposes(0)
+            read_gamma()
+            for pair in pairs:
+                token_regroup(0, pair, by_vector)
+            token_codes(0)
+            grouped = centre_regroup(flipped, by_vector)
+            centre_codes(0, grouped)
+            centre_squares(0)
+            flipped = centre_transposes(1)
+            grouped = centre_regroup(flipped, by_scalar)
+            spread_squares(0)
+            keep_squares(0)
+            centre_squares(1)
+            token_transposes(1, 0)
+            for t in range(PACK):
+                first_matmul(0, t)
+            token_transposes(1, 1)
+
+            for u in range(drain):
+                j, g, start, width = units[u]
+                if g == 0 and u > 0:
+                    for pair in pairs:
+                        token_transposes(j + 1, pair)
+                    token_regroup(j + 1, 1, by_scalar)
+                for t in range(PACK):
+                    if t == PACK - 1 and u > 0:
+                        bound(u - 1, 0)
+                    distance(u, t)
+                    if u > 0:
+                        first_matmul(u + 1, t)
+                    if g == 1 and t == 2:
+                        spread_squares(j + 1)
+                exponential(u)
+                if u > 0:
+                    quantise(u - 1, 0)
+                if u == 0:
+                    for pair in pairs:
+                        token_regroup(1, pair, by_vector)
+                    centre_codes(1, grouped)
+                    for t in range(PACK):
+                        first_matmul(1, t)
+                    token_codes(1)
+                    token_squares(1)
+                elif g == 0:
+                    token_regroup(j + 1, 0, by_vector)
+                    token_codes(j + 1)
+                    for b in banks[:4]:
+                        second_matmul(j - 1, b)
+                    for b in banks[:4]:
+                        empty(by_scalar, j - 1, b)
+                else:
+                    keep_squares(j + 1)
+                    if j > 0:
+                        for b in banks[4:]:
+                            second_matmul(j - 1, b)
+                        for b in banks[4:]:
+                            empty(by_vector if b in VECTOR_BANKS else by_scalar, j - 1, b)
+                    if j + 2 < CHUNKS:
+                        token_squares(j + 2)
+
+            left = [(j, b) for j in (CHUNKS - 2, CHUNKS - 1) for b in banks]
+            issued = 0
+            by_turn = 0
+            for u in range(drain, len(units)):
+                for t in range(PACK):
+                    if t == PACK - 1:
+                        bound(u - 1, 0)
+                    distance(u, t)
+                    if u + 1 < len(units):
+                        first_matmul(u + 1, t)
+                exponential(u)
+                quantise(u - 1, 0)
+                upto = min(issued + (4 if u == drain else 3), 12)
+                for j, b in left[issued:upto]:
+                    second_matmul(j, b)
+                issued = upto
+                if u > drain:
+                    empty(by_vector, *left[by_turn])
+                    by_turn += 1
+                for j, b in left[by_turn : by_turn + 2]:
+                    empty(by_scalar, j, b)
+                by_turn += 2
+            u = len(units) - 1
+            for i in range(2):
+                bound(u, i * P)
+                quantise(u, i * P)
+                for j, b in left[12 + 2 * i : 14 + 2 * i]:
+                    second_matmul(j, b)
+                if i == 0:
+                    empty(by_vector, *left[11])
+            for j, b in left[12:]:
+                empty(by_vector if b % 2 == 1 else by_scalar, j, b)

@@ -82,7 +82,6 @@ def tile_nystroem_kernel(
 
         nc.vector.memset(w_scales[:].bitcast(I32), 0)
 
-        nc.scalar.dma_start(out=gamma_bf16[:], in_=gamma.partition_broadcast(P))
         for pair in range(TILES // 2):
             tiles = slice(2 * pair, 2 * pair + 2)
             nc.sync.dma_start(out=token_rows(0)[:, tiles, :], in_=chunk_rows(inputs, 0)[:, tiles, :])
@@ -90,6 +89,7 @@ def tile_nystroem_kernel(
             tiles = slice(2 * pair, 2 * pair + 2)
             nc.sync.dma_start(out=c_rows[:, 0, tiles, :], in_=c_view[0][:, tiles, :])
         nc.sync.dma_start(out=c_rows[:, 1], in_=c_view[1])
+        nc.sync.dma_start(out=gamma_bf16[:], in_=gamma.partition_broadcast(P))
         load_tokens(1)
         scale_rows = normalization_scales.bitcast(I32)
         for quadrant in range(4):
@@ -209,7 +209,7 @@ def tile_nystroem_kernel(
             j, g, start, width = units[u]
             x_codes, x_scales = tokens_of[j]
             columns = slice((g * PACK + t) * P, (g * PACK + t + 1) * P)
-            xc = psum_xc.tile([P, width], F32)
+            xc = psum_xc.tile([P, width], F32, tag="xc")
             nc.tensor.matmul_mx(
                 out=xc[:],
                 lhsT=c_codes[:, columns].bitcast(FP8X4),
@@ -276,15 +276,17 @@ def tile_nystroem_kernel(
                 in_=strip_values(u, first),
             )
 
-        def second_matmul(j, b):
+        def second_matmul(j, b, passes=range(GROUPS), pool=psum_side, tag="side"):
             i, h = divmod(b, HALVES)
             d_codes, d_scales = d_codes_of[j]
             tokens = slice(i * P, (i + 1) * P)
             columns = slice(h * BANK, (h + 1) * BANK)
-            acc = psum_side.tile([P, BANK], F32, tag="side")
-            for g in range(GROUPS):
+            if passes[0] == 0:
+                acc = pool.tile([P, BANK], F32, tag=tag)
+                bank_of[j, b] = acc
+            for g in passes:
                 nc.tensor.matmul_mx(
-                    out=acc[:],
+                    out=bank_of[j, b][:],
                     lhsT=d_codes[:, g, tokens].bitcast(FP8X4),
                     lhsT_scale=d_scales[:, g, tokens],
                     rhs=w_codes[:, g, columns].bitcast(FP8X4),
@@ -292,7 +294,6 @@ def tile_nystroem_kernel(
                     start=(g == 0),
                     stop=(g == GROUPS - 1),
                 )
-            bank_of[j, b] = acc
 
         def empty(copy, j, b):
             i, h = divmod(b, HALVES)
@@ -300,7 +301,10 @@ def tile_nystroem_kernel(
                 result = results.tile([P, CENTRES], F32)
                 result_of[j, i] = result
             copy(out=result_of[j, i][:, h * BANK : (h + 1) * BANK], in_=bank_of[j, b][:])
-            if h == HALVES - 1:
+            if j == CHUNKS - 1:
+                half = slice(h * BANK, (h + 1) * BANK)
+                nc.sync.dma_start(out=chunk_rows(out, j)[:, i, half], in_=result_of[j, i][:, half])
+            elif h == HALVES - 1:
                 nc.sync.dma_start(out=chunk_rows(out, j)[:, i, :], in_=result_of[j, i][:])
 
         by_vector = nc.vector.tensor_copy
@@ -312,7 +316,6 @@ def tile_nystroem_kernel(
             for pair in pairs:
                 token_transposes(0, pair)
             flipped = centre_transposes(0)
-            read_gamma()
             for pair in pairs:
                 token_regroup(0, pair, by_vector)
             token_codes(0)
@@ -328,6 +331,7 @@ def tile_nystroem_kernel(
             for t in range(PACK):
                 first_matmul(0, t)
             token_transposes(1, 1)
+            read_gamma()
 
             for u in range(drain):
                 j, g, start, width = units[u]
@@ -394,12 +398,13 @@ def tile_nystroem_kernel(
                     empty(by_scalar, j, b)
                 by_turn += 2
             u = len(units) - 1
+            for j, b in left[12:]:
+                second_matmul(j, b, passes=[0], pool=psum_xc, tag="xc")
             for i in range(2):
                 bound(u, i * P)
                 quantise(u, i * P)
                 for j, b in left[12 + 2 * i : 14 + 2 * i]:
-                    second_matmul(j, b)
-                if i == 0:
-                    empty(by_vector, *left[11])
+                    second_matmul(j, b, passes=[1])
+            empty(by_vector, *left[11])
             for j, b in left[12:]:
                 empty(by_vector if b % 2 == 1 else by_scalar, j, b)

@@ -28,7 +28,7 @@ WORDS = FEATURES // 2
 UNBOUNDED = 3.0e38
 RUN = 4
 
-VECTOR_BANKS = (4, 6)
+VECTOR_BANKS = (4,)
 
 FLOPS = 2 * TOKENS * CENTRES * (FEATURES + CENTRES)
 
@@ -59,7 +59,7 @@ def tile_nystroem_kernel(
     with ExitStack() as ctx:
         keep = ctx.enter_context(tc.tile_pool(name="keep", bufs=1))
         work = ctx.enter_context(tc.tile_pool(name="work", bufs=3))
-        results = ctx.enter_context(tc.tile_pool(name="results", bufs=6))
+        results = ctx.enter_context(tc.tile_pool(name="results", bufs=16))
         psum_xc = ctx.enter_context(tc.psum_pool(name="psum_xc", bufs=4))
         psum_side = ctx.enter_context(tc.psum_pool(name="psum_side", bufs=4))
 
@@ -223,7 +223,7 @@ def tile_nystroem_kernel(
 
         def distance(u, t):
             j, g, start, width = units[u]
-            if t == 0:
+            if u not in half_sq_of:
                 half_sq = work.tile([P, PACK, width], F32)
                 half_sq_of[u] = half_sq
             nc.vector.scalar_tensor_tensor(
@@ -311,6 +311,10 @@ def tile_nystroem_kernel(
         by_scalar = nc.scalar.copy
         banks = range(HALVES * TILES)
         pairs = range(TILES // 2)
+
+        def banks_in_order(u):
+            return range(PACK) if u == 0 or u % 2 == 1 else range(PACK - 1, -1, -1)
+
         with tc.manual_schedule():
             token_squares(0)
             for pair in pairs:
@@ -327,10 +331,10 @@ def tile_nystroem_kernel(
             spread_squares(0)
             keep_squares(0)
             centre_squares(1)
-            token_transposes(1, 0)
             for t in range(PACK):
                 first_matmul(0, t)
-            token_transposes(1, 1)
+            for pair in pairs:
+                token_transposes(1, pair)
             read_gamma()
 
             for u in range(drain):
@@ -338,14 +342,13 @@ def tile_nystroem_kernel(
                 if g == 0 and u > 0:
                     for pair in pairs:
                         token_transposes(j + 1, pair)
-                    token_regroup(j + 1, 1, by_scalar)
-                for t in range(PACK):
-                    if t == PACK - 1 and u > 0:
+                for n, t in enumerate(banks_in_order(u)):
+                    if n == PACK - 1 and u > 0:
                         bound(u - 1, 0)
                     distance(u, t)
                     if u > 0:
                         first_matmul(u + 1, t)
-                    if g == 1 and t == 2:
+                    if g == 1 and n == 2:
                         spread_squares(j + 1)
                 exponential(u)
                 if u > 0:
@@ -359,7 +362,8 @@ def tile_nystroem_kernel(
                     token_codes(1)
                     token_squares(1)
                 elif g == 0:
-                    token_regroup(j + 1, 0, by_vector)
+                    for pair in pairs:
+                        token_regroup(j + 1, pair, by_vector)
                     token_codes(j + 1)
                     for b in banks[:4]:
                         second_matmul(j - 1, b)
@@ -379,8 +383,8 @@ def tile_nystroem_kernel(
             issued = 0
             by_turn = 0
             for u in range(drain, len(units)):
-                for t in range(PACK):
-                    if t == PACK - 1:
+                for n, t in enumerate(banks_in_order(u)):
+                    if n == PACK - 1:
                         bound(u - 1, 0)
                     distance(u, t)
                     if u + 1 < len(units):

@@ -33,18 +33,16 @@ VECTOR_BANKS = (4,)
 FLOPS = 2 * TOKENS * CENTRES * (FEATURES + CENTRES)
 
 
-def transpose_pair(nc, psum_side, identity, rows, pair):
-    flipped = psum_side.tile([P, 2, 2 * P], F32, tag="side")
-    for s in range(2):
-        row_words = rows[:, 2 * pair + s, :].bitcast(F32)
+def transpose_tiles(nc, flipped, identity, rows):
+    for s in range(rows.shape[1]):
+        row_words = rows[:, s, :].bitcast(F32)
         for u in range(2):
             nc.tensor.transpose(flipped[:, u, s * P : (s + 1) * P], row_words[:, u:WORDS:2], identity)
-    return flipped
 
 
-def regroup_pair(copy, flipped, grouped, pair):
+def regroup(copy, flipped, grouped):
     words = grouped.rearrange("p r t -> p (r t)").bitcast(F32).rearrange("p (r u) -> p r u", u=2)
-    copy(out=words[:, pair * 2 * P : (pair + 1) * 2 * P, :], in_=flipped[:].rearrange("p u r -> p r u"))
+    copy(out=words, in_=flipped.rearrange("p u r -> p r u"))
 
 
 def sum_of_squares(nc, work, row_tile, total):
@@ -82,8 +80,7 @@ def tile_nystroem_kernel(
 
         nc.vector.memset(w_scales[:].bitcast(I32), 0)
 
-        for pair in range(TILES // 2):
-            tiles = slice(2 * pair, 2 * pair + 2)
+        for tiles in (slice(0, 1), slice(1, 2), slice(2, 4)):
             nc.sync.dma_start(out=token_rows(0)[:, tiles, :], in_=chunk_rows(inputs, 0)[:, tiles, :])
         for pair in range(PACK // 2):
             tiles = slice(2 * pair, 2 * pair + 2)
@@ -114,11 +111,11 @@ def tile_nystroem_kernel(
         highest = keep.tile([P, 1], F32)
 
         def read_gamma():
-            nc.vector.tensor_scalar_mul(out=minus_two_gamma[:], in0=gamma_bf16[:], scalar1=-2.0)
-            nc.vector.tensor_scalar(
+            nc.gpsimd.tensor_scalar_mul(out=minus_two_gamma[:], in0=gamma_bf16[:], scalar1=-2.0)
+            nc.gpsimd.tensor_scalar(
                 out=lowest[:], in0=minus_two_gamma[:], scalar1=0.0, scalar2=None, op0=ALU.is_gt
             )
-            nc.vector.tensor_scalar(
+            nc.gpsimd.tensor_scalar(
                 out=highest[:], in0=lowest[:], scalar1=UNBOUNDED, scalar2=1.0, op0=ALU.mult, op1=ALU.add
             )
 
@@ -139,13 +136,18 @@ def tile_nystroem_kernel(
                 sum_of_squares(nc, work, c_rows[:, g, t, :], c2[:, g * PACK + t : g * PACK + t + 1])
             nc.scalar.mul(out=half_c2[:, tiles], in_=c2[:, tiles], mul=0.5)
 
+        def transpose_pair(rows, pair):
+            flipped = psum_side.tile([P, 2, 2 * P], F32, tag="side")
+            transpose_tiles(nc, flipped, identity[:], rows[:, 2 * pair : 2 * pair + 2, :])
+            return flipped
+
         def centre_transposes(g):
-            return [transpose_pair(nc, psum_side, identity[:], c_rows[:, g], pair) for pair in range(PACK // 2)]
+            return [transpose_pair(c_rows[:, g], pair) for pair in range(PACK // 2)]
 
         def centre_regroup(flipped, copy):
             grouped = work.tile([P, K_PASS, PACK], BF16, align_bytes=64)
             for pair in range(PACK // 2):
-                regroup_pair(copy, flipped[pair], grouped[:], pair)
+                regroup(copy, flipped[pair][:], grouped[:, pair * 2 * P : (pair + 1) * 2 * P, :])
             return grouped
 
         def centre_codes(g, grouped):
@@ -165,21 +167,34 @@ def tile_nystroem_kernel(
             x2_of[j] = x2
 
         def token_transposes(j, pair):
-            flipped_of[j, pair] = transpose_pair(nc, psum_side, identity[:], token_rows(j), pair)
+            flipped_of[j, pair] = transpose_pair(token_rows(j), pair)
 
         def token_regroup(j, pair, copy):
             if j not in grouped_of:
                 grouped = work.tile([P, CHUNK, PACK], BF16, align_bytes=64)
                 grouped_of[j] = grouped
-            regroup_pair(copy, flipped_of[j, pair], grouped_of[j][:], pair)
+            regroup(copy, flipped_of[j, pair][:], grouped_of[j][:, pair * 2 * P : (pair + 1) * 2 * P, :])
 
-        def token_codes(j):
+        def first_tokens(copy):
+            grouped = work.tile([P, CHUNK, PACK], BF16, align_bytes=64)
+            grouped_of[0] = grouped
+            for i in range(2):
+                flipped = psum_xc.tile([P, 2, P], F32, tag="xc")
+                transpose_tiles(nc, flipped, identity[:], token_rows(0)[:, i : i + 1, :])
+                regroup(copy, flipped[:], grouped[:, i * P : (i + 1) * P, :])
+
+        def token_codes(j, parts=1):
             x_codes = work.tile([P, CHUNK], U32, align_bytes=64)
             x_scales = work.tile([P, CHUNK], U8, align_bytes=64)
-            nc.vector.quantize_mx(
-                out=x_codes[:].bitcast(FP8X4), scales=x_scales[:], in_=grouped_of[j][:].rearrange("p r t -> p (r t)")
-            )
             tokens_of[j] = (x_codes, x_scales)
+
+        def token_quantise(j, columns):
+            x_codes, x_scales = tokens_of[j]
+            nc.vector.quantize_mx(
+                out=x_codes[:, columns].bitcast(FP8X4),
+                scales=x_scales[:, columns],
+                in_=grouped_of[j][:, columns, :].rearrange("p r t -> p (r t)"),
+            )
 
         def spread_squares(j):
             spread = psum_side.tile([P, CHUNK], F32, tag="side")
@@ -317,18 +332,19 @@ def tile_nystroem_kernel(
 
         with tc.manual_schedule():
             token_squares(0)
-            for pair in pairs:
-                token_transposes(0, pair)
+            first_tokens(by_vector)
+            token_transposes(0, 1)
             flipped = centre_transposes(0)
-            for pair in pairs:
-                token_regroup(0, pair, by_vector)
             token_codes(0)
+            token_quantise(0, slice(0, 2 * P))
+            token_regroup(0, 1, by_vector)
+            token_quantise(0, slice(2 * P, CHUNK))
             grouped = centre_regroup(flipped, by_vector)
             centre_codes(0, grouped)
             centre_squares(0)
+            spread_squares(0)
             flipped = centre_transposes(1)
             grouped = centre_regroup(flipped, by_scalar)
-            spread_squares(0)
             keep_squares(0)
             centre_squares(1)
             for t in range(PACK):
@@ -343,8 +359,6 @@ def tile_nystroem_kernel(
                     for pair in pairs:
                         token_transposes(j + 1, pair)
                 for n, t in enumerate(banks_in_order(u)):
-                    if n == PACK - 1 and u > 0:
-                        bound(u - 1, 0)
                     distance(u, t)
                     if u > 0:
                         first_matmul(u + 1, t)
@@ -352,6 +366,11 @@ def tile_nystroem_kernel(
                         spread_squares(j + 1)
                 exponential(u)
                 if u > 0:
+                    bound(u - 1, 0)
+                    if g == 0:
+                        token_regroup(j + 1, 0, by_vector)
+                    else:
+                        keep_squares(j + 1)
                     quantise(u - 1, 0)
                 if u == 0:
                     for pair in pairs:
@@ -360,17 +379,17 @@ def tile_nystroem_kernel(
                     for t in range(PACK):
                         first_matmul(1, t)
                     token_codes(1)
+                    token_quantise(1, slice(0, CHUNK))
                     token_squares(1)
                 elif g == 0:
-                    for pair in pairs:
-                        token_regroup(j + 1, pair, by_vector)
+                    token_regroup(j + 1, 1, by_vector)
                     token_codes(j + 1)
+                    token_quantise(j + 1, slice(0, CHUNK))
                     for b in banks[:4]:
                         second_matmul(j - 1, b)
                     for b in banks[:4]:
                         empty(by_scalar, j - 1, b)
                 else:
-                    keep_squares(j + 1)
                     if j > 0:
                         for b in banks[4:]:
                             second_matmul(j - 1, b)
@@ -384,20 +403,19 @@ def tile_nystroem_kernel(
             by_turn = 0
             for u in range(drain, len(units)):
                 for n, t in enumerate(banks_in_order(u)):
-                    if n == PACK - 1:
-                        bound(u - 1, 0)
                     distance(u, t)
                     if u + 1 < len(units):
                         first_matmul(u + 1, t)
                 exponential(u)
+                bound(u - 1, 0)
+                if u > drain:
+                    empty(by_vector, *left[by_turn])
+                    by_turn += 1
                 quantise(u - 1, 0)
                 upto = min(issued + (4 if u == drain else 3), 12)
                 for j, b in left[issued:upto]:
                     second_matmul(j, b)
                 issued = upto
-                if u > drain:
-                    empty(by_vector, *left[by_turn])
-                    by_turn += 1
                 for j, b in left[by_turn : by_turn + 2]:
                     empty(by_scalar, j, b)
                 by_turn += 2

@@ -28,8 +28,11 @@ WORDS = FEATURES // 2
 UNBOUNDED = 3.0e38
 RUN = 4
 
-VECTOR_BANKS = (4,)
+BYS = ()
+VB = ((0, 4), (1, 4))
 
+MAXU = 4
+ODDCOPY = 1
 FLOPS = 2 * TOKENS * CENTRES * (FEATURES + CENTRES)
 
 
@@ -271,9 +274,9 @@ def tile_nystroem_kernel(
         def strip_values(u, first):
             return density_of[u][:, first * PACK : (first + strip_of(u)) * PACK]
 
-        def bound(u, first):
+        def bound(u, first, engine):
             values = strip_values(u, first)
-            nc.vector.tensor_scalar(
+            engine.tensor_scalar(
                 out=values, in0=values, scalar1=highest[:, 0:1], scalar2=lowest[:, 0:1], op0=ALU.min, op1=ALU.max
             )
 
@@ -358,19 +361,29 @@ def tile_nystroem_kernel(
                 if g == 0 and u > 0:
                     for pair in pairs:
                         token_transposes(j + 1, pair)
+                    for pair in pairs:
+                        if (j + 1, pair) in BYS:
+                            token_regroup(j + 1, pair, by_scalar)
                 for n, t in enumerate(banks_in_order(u)):
                     distance(u, t)
                     if u > 0:
                         first_matmul(u + 1, t)
                     if g == 1 and n == 2:
                         spread_squares(j + 1)
+                if ODDCOPY and g == 1 and j > 0:
+                    second_matmul(j - 1, 4)
                 exponential(u)
+                if u <= MAXU:
+                    bound(u, 0, nc.gpsimd)
                 if u > 0:
-                    bound(u - 1, 0)
                     if g == 0:
-                        token_regroup(j + 1, 0, by_vector)
+                        for pair in pairs:
+                            if (j + 1, pair) not in BYS:
+                                token_regroup(j + 1, pair, by_vector)
                     else:
                         keep_squares(j + 1)
+                        if ODDCOPY and j > 0:
+                            empty(by_vector, j - 1, 4)
                     quantise(u - 1, 0)
                 if u == 0:
                     for pair in pairs:
@@ -382,7 +395,6 @@ def tile_nystroem_kernel(
                     token_quantise(1, slice(0, CHUNK))
                     token_squares(1)
                 elif g == 0:
-                    token_regroup(j + 1, 1, by_vector)
                     token_codes(j + 1)
                     token_quantise(j + 1, slice(0, CHUNK))
                     for b in banks[:4]:
@@ -391,10 +403,10 @@ def tile_nystroem_kernel(
                         empty(by_scalar, j - 1, b)
                 else:
                     if j > 0:
-                        for b in banks[4:]:
+                        for b in banks[4 + ODDCOPY :]:
                             second_matmul(j - 1, b)
-                        for b in banks[4:]:
-                            empty(by_vector if b in VECTOR_BANKS else by_scalar, j - 1, b)
+                        for b in banks[4 + ODDCOPY :]:
+                            empty(by_vector if (j - 1, b) in VB else by_scalar, j - 1, b)
                     if j + 2 < CHUNKS:
                         token_squares(j + 2)
 
@@ -407,7 +419,8 @@ def tile_nystroem_kernel(
                     if u + 1 < len(units):
                         first_matmul(u + 1, t)
                 exponential(u)
-                bound(u - 1, 0)
+                if u - 1 > MAXU:
+                    bound(u - 1, 0, nc.vector)
                 if u > drain:
                     empty(by_vector, *left[by_turn])
                     by_turn += 1
@@ -423,7 +436,7 @@ def tile_nystroem_kernel(
             for j, b in left[12:]:
                 second_matmul(j, b, passes=[0], pool=psum_xc, tag="xc")
             for i in range(2):
-                bound(u, i * P)
+                bound(u, i * P, nc.vector)
                 quantise(u, i * P)
                 for j, b in left[12 + 2 * i : 14 + 2 * i]:
                     second_matmul(j, b, passes=[1])

@@ -20,19 +20,25 @@ BANK = 512
 TOKENS, FEATURES, CENTRES = 2048, 512, 1024
 CHUNK = 512
 CHUNKS = TOKENS // CHUNK
+LAST = CHUNKS - 1
 TILES = CHUNK // P
+PAIRS = range(TILES // 2)
+PAIR = 2 * P
 GROUPS = CENTRES // K_PASS
 HALVES = CENTRES // BANK
+BANKS = range(HALVES * TILES)
 WORDS = FEATURES // 2
 
 UNBOUNDED = 3.0e38
 RUN = 4
+STRIP = 256
 
-BYS = ()
-VB = ((0, 4), (1, 4))
+SIDE_BANKS = 4
 
-MAXU = 4
-ODDCOPY = 1
+REGROUPED_IN = {0: 1, 1: 2, 4: 3}
+VECTOR_SQUARES_IN = {2: TILES - 1, 3: TILES - 2}
+VECTOR_BANK = 4
+
 FLOPS = 2 * TOKENS * CENTRES * (FEATURES + CENTRES)
 
 
@@ -48,21 +54,30 @@ def regroup(copy, flipped, grouped):
     copy(out=words, in_=flipped.rearrange("p u r -> p r u"))
 
 
-def sum_of_squares(nc, work, row_tile, total):
+def squares_by_scalar(nc, work, row_tile, total):
     squares = work.tile([P, FEATURES], BF16)
     nc.scalar.activation(out=squares[:], in_=row_tile, func=ACT.Square, accum_out=total)
+
+
+def squares_by_vector(nc, work, row_tile, total):
+    products = work.tile([P, FEATURES], F32)
+    nc.vector.scalar_tensor_tensor(
+        out=products[:], in0=row_tile, scalar=1.0, in1=row_tile, op0=ALU.mult, op1=ALU.mult, accum_out=total
+    )
 
 
 def tile_nystroem_kernel(
     tc, inputs, centers, gamma, normalization_words, normalization_scales, out
 ):
     nc = tc.nc
+    by_vector = nc.vector.tensor_copy
+    by_scalar = nc.scalar.copy
     with ExitStack() as ctx:
         keep = ctx.enter_context(tc.tile_pool(name="keep", bufs=1))
         work = ctx.enter_context(tc.tile_pool(name="work", bufs=3))
-        results = ctx.enter_context(tc.tile_pool(name="results", bufs=16))
-        psum_xc = ctx.enter_context(tc.psum_pool(name="psum_xc", bufs=4))
-        psum_side = ctx.enter_context(tc.psum_pool(name="psum_side", bufs=4))
+        results = ctx.enter_context(tc.tile_pool(name="results", bufs=TOKENS // P))
+        psum_xc = ctx.enter_context(tc.psum_pool(name="psum_xc", bufs=PACK))
+        psum_side = ctx.enter_context(tc.psum_pool(name="psum_side", bufs=SIDE_BANKS))
 
         c_view = centers.rearrange("(g p t) d -> g p t d", p=P, t=PACK)
 
@@ -83,9 +98,9 @@ def tile_nystroem_kernel(
 
         nc.vector.memset(w_scales[:].bitcast(I32), 0)
 
-        for tiles in (slice(0, 1), slice(1, 2), slice(2, 4)):
+        for tiles in (slice(0, 1), slice(1, 2), slice(2, TILES)):
             nc.sync.dma_start(out=token_rows(0)[:, tiles, :], in_=chunk_rows(inputs, 0)[:, tiles, :])
-        for pair in range(PACK // 2):
+        for pair in PAIRS:
             tiles = slice(2 * pair, 2 * pair + 2)
             nc.sync.dma_start(out=c_rows[:, 0, tiles, :], in_=c_view[0][:, tiles, :])
         nc.sync.dma_start(out=c_rows[:, 1], in_=c_view[1])
@@ -127,76 +142,72 @@ def tile_nystroem_kernel(
         c2 = keep.tile([P, GROUPS * PACK], F32)
         half_c2 = keep.tile([P, GROUPS * PACK], F32)
 
-        flipped_of = {}
-        grouped_of = {}
-        x2_of = {}
-        spread_of = {}
-        tokens_of = {}
+        def transpose_pair(rows, pair):
+            flipped = psum_side.tile([P, 2, PAIR], F32, tag="side")
+            transpose_tiles(nc, flipped, identity[:], rows[:, 2 * pair : 2 * pair + 2, :])
+            return flipped
+
+        def columns_of(pair):
+            return slice(pair * PAIR, (pair + 1) * PAIR)
 
         def centre_squares(g):
             tiles = slice(g * PACK, (g + 1) * PACK)
             for t in range(PACK):
-                sum_of_squares(nc, work, c_rows[:, g, t, :], c2[:, g * PACK + t : g * PACK + t + 1])
+                squares_by_scalar(nc, work, c_rows[:, g, t, :], c2[:, g * PACK + t : g * PACK + t + 1])
             nc.scalar.mul(out=half_c2[:, tiles], in_=c2[:, tiles], mul=0.5)
 
-        def transpose_pair(rows, pair):
-            flipped = psum_side.tile([P, 2, 2 * P], F32, tag="side")
-            transpose_tiles(nc, flipped, identity[:], rows[:, 2 * pair : 2 * pair + 2, :])
-            return flipped
-
-        def centre_transposes(g):
-            return [transpose_pair(c_rows[:, g], pair) for pair in range(PACK // 2)]
-
-        def centre_regroup(flipped, copy):
+        def centre_regroup(g, copy):
+            banks = [transpose_pair(c_rows[:, g], pair) for pair in PAIRS]
             grouped = work.tile([P, K_PASS, PACK], BF16, align_bytes=64)
-            for pair in range(PACK // 2):
-                regroup(copy, flipped[pair][:], grouped[:, pair * 2 * P : (pair + 1) * 2 * P, :])
+            for pair in PAIRS:
+                regroup(copy, banks[pair][:], grouped[:, columns_of(pair), :])
             return grouped
 
         def centre_codes(g, grouped):
-            for pair in range(PACK // 2):
-                first = g * K_PASS + pair * 2 * P
-                columns = slice(first, first + 2 * P)
+            for pair in PAIRS:
+                columns = slice(g * K_PASS + pair * PAIR, g * K_PASS + (pair + 1) * PAIR)
                 nc.vector.quantize_mx(
                     out=c_codes[:, columns].bitcast(FP8X4),
                     scales=c_scales[:, columns],
-                    in_=grouped[:, pair * 2 * P : (pair + 1) * 2 * P, :].rearrange("p r t -> p (r t)"),
+                    in_=grouped[:, columns_of(pair), :].rearrange("p r t -> p (r t)"),
                 )
 
-        def token_squares(j):
-            x2 = work.tile([P, TILES], F32)
-            for i in range(TILES):
-                sum_of_squares(nc, work, token_rows(j)[:, i, :], x2[:, i : i + 1])
-            x2_of[j] = x2
+        token_banks = {}
+        token_words = {}
+        token_codes = {}
+        x2_of = {}
+        spread_of = {}
+        half_x2_of = {}
 
-        def token_transposes(j, pair):
-            flipped_of[j, pair] = transpose_pair(token_rows(j), pair)
+        def token_squares(j, tiles, add_up):
+            if j not in x2_of:
+                x2 = work.tile([P, TILES], F32)
+                x2_of[j] = x2
+            for i in tiles:
+                add_up(nc, work, token_rows(j)[:, i, :], x2_of[j][:, i : i + 1])
 
-        def token_regroup(j, pair, copy):
-            if j not in grouped_of:
-                grouped = work.tile([P, CHUNK, PACK], BF16, align_bytes=64)
-                grouped_of[j] = grouped
-            regroup(copy, flipped_of[j, pair][:], grouped_of[j][:, pair * 2 * P : (pair + 1) * 2 * P, :])
-
-        def first_tokens(copy):
+        def new_token_words(j):
             grouped = work.tile([P, CHUNK, PACK], BF16, align_bytes=64)
-            grouped_of[0] = grouped
-            for i in range(2):
-                flipped = psum_xc.tile([P, 2, P], F32, tag="xc")
-                transpose_tiles(nc, flipped, identity[:], token_rows(0)[:, i : i + 1, :])
-                regroup(copy, flipped[:], grouped[:, i * P : (i + 1) * P, :])
+            token_words[j] = grouped
 
-        def token_codes(j, parts=1):
-            x_codes = work.tile([P, CHUNK], U32, align_bytes=64)
-            x_scales = work.tile([P, CHUNK], U8, align_bytes=64)
-            tokens_of[j] = (x_codes, x_scales)
+        def token_transposes(j):
+            token_banks[j] = [transpose_pair(token_rows(j), pair) for pair in PAIRS]
+
+        def token_regroup(j, pair):
+            if j not in token_words:
+                new_token_words(j)
+            regroup(by_vector, token_banks[j][pair][:], token_words[j][:, columns_of(pair), :])
 
         def token_quantise(j, columns):
-            x_codes, x_scales = tokens_of[j]
+            if j not in token_codes:
+                x_codes = work.tile([P, CHUNK], U32, align_bytes=64)
+                x_scales = work.tile([P, CHUNK], U8, align_bytes=64)
+                token_codes[j] = (x_codes, x_scales)
+            x_codes, x_scales = token_codes[j]
             nc.vector.quantize_mx(
                 out=x_codes[:, columns].bitcast(FP8X4),
                 scales=x_scales[:, columns],
-                in_=grouped_of[j][:, columns, :].rearrange("p r t -> p (r t)"),
+                in_=token_words[j][:, columns, :].rearrange("p r t -> p (r t)"),
             )
 
         def spread_squares(j):
@@ -212,10 +223,11 @@ def tile_nystroem_kernel(
             nc.vector.tensor_scalar_mul(out=half_x2[:], in0=spread_of[j][:], scalar1=0.5)
             half_x2_of[j] = half_x2
 
-        units = [(j, g, 0, CHUNK) for j in range(CHUNKS - 1) for g in range(GROUPS)]
+        units = [(j, g, 0, CHUNK) for j in range(LAST) for g in range(GROUPS)]
         drain = len(units)
-        units += [(CHUNKS - 1, g, first, CHUNK // 2) for first in (0, CHUNK // 2) for g in range(GROUPS)]
-        half_x2_of = {}
+        units += [(LAST, g, first, CHUNK // 2) for first in (0, CHUNK // 2) for g in range(GROUPS)]
+        final = len(units) - 1
+
         xc_of = {}
         half_sq_of = {}
         density_of = {}
@@ -225,7 +237,7 @@ def tile_nystroem_kernel(
 
         def first_matmul(u, t):
             j, g, start, width = units[u]
-            x_codes, x_scales = tokens_of[j]
+            x_codes, x_scales = token_codes[j]
             columns = slice((g * PACK + t) * P, (g * PACK + t + 1) * P)
             xc = psum_xc.tile([P, width], F32, tag="xc")
             nc.tensor.matmul_mx(
@@ -238,6 +250,9 @@ def tile_nystroem_kernel(
                 stop=True,
             )
             xc_of[u, t] = xc
+
+        def reading_order(u):
+            return range(PACK) if u == 0 or u % 2 == 1 else range(PACK - 1, -1, -1)
 
         def distance(u, t):
             j, g, start, width = units[u]
@@ -253,193 +268,184 @@ def tile_nystroem_kernel(
                 op1=ALU.subtract,
             )
 
-        def exponential(u):
+        def strips(u):
             width = units[u][3]
-            densities = work.tile([P, width * PACK], BF16, align_bytes=64)
-            for first in range(0, width, strip_of(u)):
-                strip = slice(first, first + strip_of(u))
+            step = P if u == final else STRIP
+            return [slice(first, first + step) for first in range(0, width, step)]
+
+        def values_of(u, strip):
+            return density_of[u][:, strip.start * PACK : strip.stop * PACK]
+
+        def exponential(u):
+            densities = work.tile([P, units[u][3] * PACK], BF16, align_bytes=64)
+            density_of[u] = densities
+            for strip in strips(u):
                 nc.scalar.activation(
-                    out=densities[:, first * PACK : strip.stop * PACK].rearrange(
-                        "p (c i t) -> p c t i", i=RUN, t=PACK
-                    ),
+                    out=values_of(u, strip).rearrange("p (c i t) -> p c t i", i=RUN, t=PACK),
                     in_=half_sq_of[u][:, :, strip].rearrange("p t (c i) -> p c t i", i=RUN),
                     func=ACT.Exp,
                     scale=minus_two_gamma[:, 0:1],
                 )
-            density_of[u] = densities
 
-        def strip_of(u):
-            return P if u == len(units) - 1 else units[u][3]
-
-        def strip_values(u, first):
-            return density_of[u][:, first * PACK : (first + strip_of(u)) * PACK]
-
-        def bound(u, first, engine):
-            values = strip_values(u, first)
+        def bound(engine, u, strip):
+            values = values_of(u, strip)
             engine.tensor_scalar(
                 out=values, in0=values, scalar1=highest[:, 0:1], scalar2=lowest[:, 0:1], op0=ALU.min, op1=ALU.max
             )
 
-        def quantise(u, first):
+        def quantise(u, strip):
             j, g, start, width = units[u]
             if j not in d_codes_of:
                 d_codes = work.tile([P, GROUPS, CHUNK], U32, align_bytes=64)
                 d_scales = work.tile([P, GROUPS, CHUNK], U8, align_bytes=64)
                 d_codes_of[j] = (d_codes, d_scales)
             d_codes, d_scales = d_codes_of[j]
-            tokens = slice(start + first, start + first + strip_of(u))
+            tokens = slice(start + strip.start, start + strip.stop)
             nc.vector.quantize_mx(
-                out=d_codes[:, g, tokens].bitcast(FP8X4),
-                scales=d_scales[:, g, tokens],
-                in_=strip_values(u, first),
+                out=d_codes[:, g, tokens].bitcast(FP8X4), scales=d_scales[:, g, tokens], in_=values_of(u, strip)
             )
 
-        def second_matmul(j, b, passes=range(GROUPS), pool=psum_side, tag="side"):
+        def whole(u):
+            return slice(0, units[u][3])
+
+        def second_bank(pool, tag, j, b):
+            acc = pool.tile([P, BANK], F32, tag=tag)
+            bank_of[j, b] = acc
+
+        def second_pass(j, b, g):
             i, h = divmod(b, HALVES)
             d_codes, d_scales = d_codes_of[j]
             tokens = slice(i * P, (i + 1) * P)
             columns = slice(h * BANK, (h + 1) * BANK)
-            if passes[0] == 0:
-                acc = pool.tile([P, BANK], F32, tag=tag)
-                bank_of[j, b] = acc
-            for g in passes:
-                nc.tensor.matmul_mx(
-                    out=bank_of[j, b][:],
-                    lhsT=d_codes[:, g, tokens].bitcast(FP8X4),
-                    lhsT_scale=d_scales[:, g, tokens],
-                    rhs=w_codes[:, g, columns].bitcast(FP8X4),
-                    rhs_scale=w_scales[:, g, columns],
-                    start=(g == 0),
-                    stop=(g == GROUPS - 1),
-                )
+            nc.tensor.matmul_mx(
+                out=bank_of[j, b][:],
+                lhsT=d_codes[:, g, tokens].bitcast(FP8X4),
+                lhsT_scale=d_scales[:, g, tokens],
+                rhs=w_codes[:, g, columns].bitcast(FP8X4),
+                rhs_scale=w_scales[:, g, columns],
+                start=(g == 0),
+                stop=(g == GROUPS - 1),
+            )
+
+        def second_matmul(j, b):
+            second_bank(psum_side, "side", j, b)
+            for g in range(GROUPS):
+                second_pass(j, b, g)
 
         def empty(copy, j, b):
             i, h = divmod(b, HALVES)
             if h == 0:
                 result = results.tile([P, CENTRES], F32)
                 result_of[j, i] = result
-            copy(out=result_of[j, i][:, h * BANK : (h + 1) * BANK], in_=bank_of[j, b][:])
-            if j == CHUNKS - 1:
-                half = slice(h * BANK, (h + 1) * BANK)
+            half = slice(h * BANK, (h + 1) * BANK)
+            copy(out=result_of[j, i][:, half], in_=bank_of[j, b][:])
+            if j == LAST:
                 nc.sync.dma_start(out=chunk_rows(out, j)[:, i, half], in_=result_of[j, i][:, half])
             elif h == HALVES - 1:
                 nc.sync.dma_start(out=chunk_rows(out, j)[:, i, :], in_=result_of[j, i][:])
 
-        by_vector = nc.vector.tensor_copy
-        by_scalar = nc.scalar.copy
-        banks = range(HALVES * TILES)
-        pairs = range(TILES // 2)
-
-        def banks_in_order(u):
-            return range(PACK) if u == 0 or u % 2 == 1 else range(PACK - 1, -1, -1)
-
         with tc.manual_schedule():
-            token_squares(0)
-            first_tokens(by_vector)
-            token_transposes(0, 1)
-            flipped = centre_transposes(0)
-            token_codes(0)
-            token_quantise(0, slice(0, 2 * P))
-            token_regroup(0, 1, by_vector)
-            token_quantise(0, slice(2 * P, CHUNK))
-            grouped = centre_regroup(flipped, by_vector)
-            centre_codes(0, grouped)
+            token_squares(0, range(TILES), squares_by_scalar)
+            new_token_words(0)
+            for i in range(2):
+                flipped = psum_xc.tile([P, 2, P], F32, tag="xc")
+                transpose_tiles(nc, flipped, identity[:], token_rows(0)[:, i : i + 1, :])
+                regroup(by_vector, flipped[:], token_words[0][:, i * P : (i + 1) * P, :])
+            second_pair = transpose_pair(token_rows(0), 1)
+            token_quantise(0, columns_of(0))
+            regroup(by_vector, second_pair[:], token_words[0][:, columns_of(1), :])
+            token_quantise(0, columns_of(1))
+            centre_codes(0, centre_regroup(0, by_vector))
             centre_squares(0)
             spread_squares(0)
-            flipped = centre_transposes(1)
-            grouped = centre_regroup(flipped, by_scalar)
+            centre_words = centre_regroup(1, by_scalar)
             keep_squares(0)
             centre_squares(1)
             for t in range(PACK):
                 first_matmul(0, t)
-            for pair in pairs:
-                token_transposes(1, pair)
+            token_transposes(1)
             read_gamma()
 
             for u in range(drain):
                 j, g, start, width = units[u]
-                if g == 0 and u > 0:
-                    for pair in pairs:
-                        token_transposes(j + 1, pair)
-                    for pair in pairs:
-                        if (j + 1, pair) in BYS:
-                            token_regroup(j + 1, pair, by_scalar)
-                for n, t in enumerate(banks_in_order(u)):
+                if u > 0 and u in REGROUPED_IN:
+                    token_transposes(REGROUPED_IN[u])
+                if g == 1:
+                    spread_squares(j + 1)
+                for t in reading_order(u):
                     distance(u, t)
                     if u > 0:
                         first_matmul(u + 1, t)
-                    if g == 1 and n == 2:
-                        spread_squares(j + 1)
-                if ODDCOPY and g == 1 and j > 0:
-                    second_matmul(j - 1, 4)
                 exponential(u)
-                if u <= MAXU:
-                    bound(u, 0, nc.gpsimd)
+                if u + 1 < drain:
+                    for strip in strips(u):
+                        bound(nc.gpsimd, u, strip)
+                if u in REGROUPED_IN:
+                    token_regroup(REGROUPED_IN[u], 0)
+                elif g == 1:
+                    keep_squares(j + 1)
                 if u > 0:
-                    if g == 0:
-                        for pair in pairs:
-                            if (j + 1, pair) not in BYS:
-                                token_regroup(j + 1, pair, by_vector)
-                    else:
+                    quantise(u - 1, whole(u - 1))
+                if u in REGROUPED_IN:
+                    token_regroup(REGROUPED_IN[u], 1)
+                    if g == 1:
                         keep_squares(j + 1)
-                        if ODDCOPY and j > 0:
-                            empty(by_vector, j - 1, 4)
-                    quantise(u - 1, 0)
+                if g == 1 and u in VECTOR_SQUARES_IN:
+                    token_squares(LAST, [VECTOR_SQUARES_IN[u]], squares_by_vector)
                 if u == 0:
-                    for pair in pairs:
-                        token_regroup(1, pair, by_vector)
-                    centre_codes(1, grouped)
+                    centre_codes(1, centre_words)
                     for t in range(PACK):
                         first_matmul(1, t)
-                    token_codes(1)
                     token_quantise(1, slice(0, CHUNK))
-                    token_squares(1)
+                    token_squares(1, range(TILES), squares_by_scalar)
                 elif g == 0:
-                    token_codes(j + 1)
                     token_quantise(j + 1, slice(0, CHUNK))
-                    for b in banks[:4]:
+                    if u in VECTOR_SQUARES_IN:
+                        token_squares(LAST, [VECTOR_SQUARES_IN[u]], squares_by_vector)
+                    for b in BANKS[:SIDE_BANKS]:
                         second_matmul(j - 1, b)
-                    for b in banks[:4]:
+                    for b in BANKS[:SIDE_BANKS]:
                         empty(by_scalar, j - 1, b)
                 else:
                     if j > 0:
-                        for b in banks[4 + ODDCOPY :]:
+                        for b in BANKS[SIDE_BANKS:]:
                             second_matmul(j - 1, b)
-                        for b in banks[4 + ODDCOPY :]:
-                            empty(by_vector if (j - 1, b) in VB else by_scalar, j - 1, b)
-                    if j + 2 < CHUNKS:
-                        token_squares(j + 2)
+                        for b in BANKS[SIDE_BANKS:]:
+                            empty(by_vector if b == VECTOR_BANK else by_scalar, j - 1, b)
+                    if j + 2 <= LAST:
+                        by_others = len(VECTOR_SQUARES_IN) if j + 2 == LAST else 0
+                        token_squares(j + 2, range(TILES - by_others), squares_by_scalar)
 
-            left = [(j, b) for j in (CHUNKS - 2, CHUNKS - 1) for b in banks]
+            left = [(j, b) for j in (LAST - 1, LAST) for b in BANKS]
+            ready = len(left) - 4
             issued = 0
-            by_turn = 0
+            emptied = 0
             for u in range(drain, len(units)):
-                for n, t in enumerate(banks_in_order(u)):
+                for t in reading_order(u):
                     distance(u, t)
-                    if u + 1 < len(units):
+                    if u < final:
                         first_matmul(u + 1, t)
                 exponential(u)
-                if u - 1 > MAXU:
-                    bound(u - 1, 0, nc.vector)
+                for strip in strips(u - 1):
+                    bound(nc.vector, u - 1, strip)
                 if u > drain:
-                    empty(by_vector, *left[by_turn])
-                    by_turn += 1
-                quantise(u - 1, 0)
-                upto = min(issued + (4 if u == drain else 3), 12)
+                    empty(by_vector, *left[emptied])
+                    emptied += 1
+                quantise(u - 1, whole(u - 1))
+                upto = min(issued + (SIDE_BANKS if u == drain else 3), ready)
                 for j, b in left[issued:upto]:
                     second_matmul(j, b)
                 issued = upto
-                for j, b in left[by_turn : by_turn + 2]:
+                for j, b in left[emptied : emptied + 2]:
                     empty(by_scalar, j, b)
-                by_turn += 2
-            u = len(units) - 1
-            for j, b in left[12:]:
-                second_matmul(j, b, passes=[0], pool=psum_xc, tag="xc")
-            for i in range(2):
-                bound(u, i * P, nc.vector)
-                quantise(u, i * P)
-                for j, b in left[12 + 2 * i : 14 + 2 * i]:
-                    second_matmul(j, b, passes=[1])
-            empty(by_vector, *left[11])
-            for j, b in left[12:]:
-                empty(by_vector if b % 2 == 1 else by_scalar, j, b)
+                emptied += 2
+            for j, b in left[ready:]:
+                second_bank(psum_xc, "xc", j, b)
+                second_pass(j, b, 0)
+            for n, strip in enumerate(strips(final)):
+                bound(nc.vector, final, strip)
+                quantise(final, strip)
+                for j, b in left[ready + HALVES * n : ready + HALVES * (n + 1)]:
+                    second_pass(j, b, 1)
+            for n, (j, b) in enumerate(left[emptied:]):
+                empty(by_vector if n % 2 == 0 else by_scalar, j, b)

from contextlib import ExitStack

import concourse.mybir as mybir
from concourse.masks import make_identity

F32 = mybir.dt.float32
BF16 = mybir.dt.bfloat16
I32 = mybir.dt.int32
U32 = mybir.dt.uint32
U8 = mybir.dt.uint8
FP8X4 = mybir.dt.float8_e4m3fn_x4
ALU = mybir.AluOpType
ACT = mybir.ActivationFunctionType

P = 128
PACK = 4
K_PASS = P * PACK
BANK = 512

TOKENS, FEATURES, CENTRES = 2048, 512, 1024
CHUNK = 512
CHUNKS = TOKENS // CHUNK
LAST = CHUNKS - 1
TILES = CHUNK // P
PAIRS = range(TILES // 2)
PAIR = 2 * P
GROUPS = CENTRES // K_PASS
HALVES = CENTRES // BANK
BANKS = range(HALVES * TILES)
WORDS = FEATURES // 2

UNBOUNDED = 3.0e38
RUN = 4
STRIP = 256

SIDE_BANKS = 4

REGROUPED_IN = {0: 1, 1: 2, 4: 3}
VECTOR_SQUARES_IN = {2: TILES - 1, 3: TILES - 2}
VECTOR_BANK = 4

FLOPS = 2 * TOKENS * CENTRES * (FEATURES + CENTRES)


def transpose_tiles(nc, flipped, identity, rows):
    for s in range(rows.shape[1]):
        row_words = rows[:, s, :].bitcast(F32)
        for u in range(2):
            nc.tensor.transpose(flipped[:, u, s * P : (s + 1) * P], row_words[:, u:WORDS:2], identity)


def regroup(copy, flipped, grouped):
    words = grouped.rearrange("p r t -> p (r t)").bitcast(F32).rearrange("p (r u) -> p r u", u=2)
    copy(out=words, in_=flipped.rearrange("p u r -> p r u"))


def squares_by_scalar(nc, work, row_tile, total):
    squares = work.tile([P, FEATURES], BF16)
    nc.scalar.activation(out=squares[:], in_=row_tile, func=ACT.Square, accum_out=total)


def squares_by_vector(nc, work, row_tile, total):
    products = work.tile([P, FEATURES], F32)
    nc.vector.scalar_tensor_tensor(
        out=products[:], in0=row_tile, scalar=1.0, in1=row_tile, op0=ALU.mult, op1=ALU.mult, accum_out=total
    )


def tile_nystroem_kernel(
    tc, inputs, centers, gamma, normalization_words, normalization_scales, out
):
    nc = tc.nc
    by_vector = nc.vector.tensor_copy
    by_scalar = nc.scalar.copy
    with ExitStack() as ctx:
        keep = ctx.enter_context(tc.tile_pool(name="keep", bufs=1))
        work = ctx.enter_context(tc.tile_pool(name="work", bufs=3))
        results = ctx.enter_context(tc.tile_pool(name="results", bufs=TOKENS // P))
        psum_xc = ctx.enter_context(tc.psum_pool(name="psum_xc", bufs=PACK))
        psum_side = ctx.enter_context(tc.psum_pool(name="psum_side", bufs=SIDE_BANKS))

        c_view = centers.rearrange("(g p t) d -> g p t d", p=P, t=PACK)

        def chunk_rows(tensor, j):
            return tensor[j * CHUNK : (j + 1) * CHUNK, :].rearrange("(p i) d -> p i d", p=P)

        def token_rows(j):
            return x_rows[:, j * TILES : (j + 1) * TILES, :]

        def load_tokens(j):
            nc.sync.dma_start(out=token_rows(j), in_=chunk_rows(inputs, j))

        x_rows = keep.tile([P, TOKENS // P, FEATURES], BF16)
        c_rows = keep.tile([P, GROUPS, PACK, FEATURES], BF16)
        gamma_bf16 = keep.tile([P, 1], BF16)
        w_codes = keep.tile([P, GROUPS, CENTRES], U32, align_bytes=64)
        w_scales = keep.tile([P, GROUPS, CENTRES], U8, align_bytes=64)

        nc.vector.memset(w_scales[:].bitcast(I32), 0)

        for tiles in (slice(0, 1), slice(1, 2), slice(2, TILES)):
            nc.sync.dma_start(out=token_rows(0)[:, tiles, :], in_=chunk_rows(inputs, 0)[:, tiles, :])
        for pair in PAIRS:
            tiles = slice(2 * pair, 2 * pair + 2)
            nc.sync.dma_start(out=c_rows[:, 0, tiles, :], in_=c_view[0][:, tiles, :])
        nc.sync.dma_start(out=c_rows[:, 1], in_=c_view[1])
        nc.sync.dma_start(out=gamma_bf16[:], in_=gamma.partition_broadcast(P))
        load_tokens(1)
        scale_rows = normalization_scales.bitcast(I32)
        for quadrant in range(4):
            nc.sync.dma_start(
                out=w_scales[32 * quadrant : 32 * quadrant + 4].bitcast(I32),
                in_=scale_rows[:, 4 * quadrant : 4 * quadrant + 4, :].rearrange("g r n -> r g n"),
            )
        word_rows = normalization_words.rearrange("g p n t -> g p (n t)").bitcast(I32)
        for g in range(GROUPS):
            nc.sync.dma_start(out=w_codes[:, g, :].bitcast(I32), in_=word_rows[g])
        for j in range(2, CHUNKS):
            load_tokens(j)

        identity = keep.tile([P, P], F32)
        make_identity(nc, identity[:])
        zero = keep.tile([P, 1], F32)
        one = keep.tile([P, 1], F32)
        nc.vector.memset(zero[:], 0.0)
        nc.scalar.activation(out=one[:], in_=zero[:], func=ACT.Exp)
        minus_two_gamma = keep.tile([P, 1], F32)
        lowest = keep.tile([P, 1], F32)
        highest = keep.tile([P, 1], F32)

        def read_gamma():
            nc.gpsimd.tensor_scalar_mul(out=minus_two_gamma[:], in0=gamma_bf16[:], scalar1=-2.0)
            nc.gpsimd.tensor_scalar(
                out=lowest[:], in0=minus_two_gamma[:], scalar1=0.0, scalar2=None, op0=ALU.is_gt
            )
            nc.gpsimd.tensor_scalar(
                out=highest[:], in0=lowest[:], scalar1=UNBOUNDED, scalar2=1.0, op0=ALU.mult, op1=ALU.add
            )

        c_codes = keep.tile([P, CENTRES], U32, align_bytes=64)
        c_scales = keep.tile([P, CENTRES], U8, align_bytes=64)
        c2 = keep.tile([P, GROUPS * PACK], F32)
        half_c2 = keep.tile([P, GROUPS * PACK], F32)

        def transpose_pair(rows, pair):
            flipped = psum_side.tile([P, 2, PAIR], F32, tag="side")
            transpose_tiles(nc, flipped, identity[:], rows[:, 2 * pair : 2 * pair + 2, :])
            return flipped

        def columns_of(pair):
            return slice(pair * PAIR, (pair + 1) * PAIR)

        def centre_squares(g):
            tiles = slice(g * PACK, (g + 1) * PACK)
            for t in range(PACK):
                squares_by_scalar(nc, work, c_rows[:, g, t, :], c2[:, g * PACK + t : g * PACK + t + 1])
            nc.scalar.mul(out=half_c2[:, tiles], in_=c2[:, tiles], mul=0.5)

        def centre_regroup(g, copy):
            banks = [transpose_pair(c_rows[:, g], pair) for pair in PAIRS]
            grouped = work.tile([P, K_PASS, PACK], BF16, align_bytes=64)
            for pair in PAIRS:
                regroup(copy, banks[pair][:], grouped[:, columns_of(pair), :])
            return grouped

        def centre_codes(g, grouped):
            for pair in PAIRS:
                columns = slice(g * K_PASS + pair * PAIR, g * K_PASS + (pair + 1) * PAIR)
                nc.vector.quantize_mx(
                    out=c_codes[:, columns].bitcast(FP8X4),
                    scales=c_scales[:, columns],
                    in_=grouped[:, columns_of(pair), :].rearrange("p r t -> p (r t)"),
                )

        token_banks = {}
        token_words = {}
        token_codes = {}
        x2_of = {}
        spread_of = {}
        half_x2_of = {}

        def token_squares(j, tiles, add_up):
            if j not in x2_of:
                x2 = work.tile([P, TILES], F32)
                x2_of[j] = x2
            for i in tiles:
                add_up(nc, work, token_rows(j)[:, i, :], x2_of[j][:, i : i + 1])

        def new_token_words(j):
            grouped = work.tile([P, CHUNK, PACK], BF16, align_bytes=64)
            token_words[j] = grouped

        def token_transposes(j):
            token_banks[j] = [transpose_pair(token_rows(j), pair) for pair in PAIRS]

        def token_regroup(j, pair):
            if j not in token_words:
                new_token_words(j)
            regroup(by_vector, token_banks[j][pair][:], token_words[j][:, columns_of(pair), :])

        def token_quantise(j, columns):
            if j not in token_codes:
                x_codes = work.tile([P, CHUNK], U32, align_bytes=64)
                x_scales = work.tile([P, CHUNK], U8, align_bytes=64)
                token_codes[j] = (x_codes, x_scales)
            x_codes, x_scales = token_codes[j]
            nc.vector.quantize_mx(
                out=x_codes[:, columns].bitcast(FP8X4),
                scales=x_scales[:, columns],
                in_=token_words[j][:, columns, :].rearrange("p r t -> p (r t)"),
            )

        def spread_squares(j):
            spread = psum_side.tile([P, CHUNK], F32, tag="side")
            for i in range(TILES):
                nc.tensor.transpose(
                    spread[:, i * P : (i + 1) * P], x2_of[j][:, i : i + 1].to_broadcast([P, P]), identity[:]
                )
            spread_of[j] = spread

        def keep_squares(j):
            half_x2 = work.tile([P, CHUNK], F32)
            nc.vector.tensor_scalar_mul(out=half_x2[:], in0=spread_of[j][:], scalar1=0.5)
            half_x2_of[j] = half_x2

        units = [(j, g, 0, CHUNK) for j in range(LAST) for g in range(GROUPS)]
        drain = len(units)
        units += [(LAST, g, first, CHUNK // 2) for first in (0, CHUNK // 2) for g in range(GROUPS)]
        final = len(units) - 1

        xc_of = {}
        half_sq_of = {}
        density_of = {}
        d_codes_of = {}
        bank_of = {}
        result_of = {}

        def first_matmul(u, t):
            j, g, start, width = units[u]
            x_codes, x_scales = token_codes[j]
            columns = slice((g * PACK + t) * P, (g * PACK + t + 1) * P)
            xc = psum_xc.tile([P, width], F32, tag="xc")
            nc.tensor.matmul_mx(
                out=xc[:],
                lhsT=c_codes[:, columns].bitcast(FP8X4),
                lhsT_scale=c_scales[:, columns],
                rhs=x_codes[:, start : start + width].bitcast(FP8X4),
                rhs_scale=x_scales[:, start : start + width],
                start=True,
                stop=True,
            )
            xc_of[u, t] = xc

        def reading_order(u):
            return range(PACK) if u == 0 or u % 2 == 1 else range(PACK - 1, -1, -1)

        def distance(u, t):
            j, g, start, width = units[u]
            if u not in half_sq_of:
                half_sq = work.tile([P, PACK, width], F32)
                half_sq_of[u] = half_sq
            nc.vector.scalar_tensor_tensor(
                out=half_sq_of[u][:, t, :],
                in0=half_x2_of[j][:, start : start + width],
                scalar=half_c2[:, g * PACK + t : g * PACK + t + 1],
                in1=xc_of[u, t][:],
                op0=ALU.add,
                op1=ALU.subtract,
            )

        def strips(u):
            width = units[u][3]
            step = P if u == final else STRIP
            return [slice(first, first + step) for first in range(0, width, step)]

        def values_of(u, strip):
            return density_of[u][:, strip.start * PACK : strip.stop * PACK]

        def exponential(u):
            densities = work.tile([P, units[u][3] * PACK], BF16, align_bytes=64)
            density_of[u] = densities
            for strip in strips(u):
                nc.scalar.activation(
                    out=values_of(u, strip).rearrange("p (c i t) -> p c t i", i=RUN, t=PACK),
                    in_=half_sq_of[u][:, :, strip].rearrange("p t (c i) -> p c t i", i=RUN),
                    func=ACT.Exp,
                    scale=minus_two_gamma[:, 0:1],
                )

        def bound(engine, u, strip):
            values = values_of(u, strip)
            engine.tensor_scalar(
                out=values, in0=values, scalar1=highest[:, 0:1], scalar2=lowest[:, 0:1], op0=ALU.min, op1=ALU.max
            )

        def quantise(u, strip):
            j, g, start, width = units[u]
            if j not in d_codes_of:
                d_codes = work.tile([P, GROUPS, CHUNK], U32, align_bytes=64)
                d_scales = work.tile([P, GROUPS, CHUNK], U8, align_bytes=64)
                d_codes_of[j] = (d_codes, d_scales)
            d_codes, d_scales = d_codes_of[j]
            tokens = slice(start + strip.start, start + strip.stop)
            nc.vector.quantize_mx(
                out=d_codes[:, g, tokens].bitcast(FP8X4), scales=d_scales[:, g, tokens], in_=values_of(u, strip)
            )

        def whole(u):
            return slice(0, units[u][3])

        def second_bank(pool, tag, j, b):
            acc = pool.tile([P, BANK], F32, tag=tag)
            bank_of[j, b] = acc

        def second_pass(j, b, g):
            i, h = divmod(b, HALVES)
            d_codes, d_scales = d_codes_of[j]
            tokens = slice(i * P, (i + 1) * P)
            columns = slice(h * BANK, (h + 1) * BANK)
            nc.tensor.matmul_mx(
                out=bank_of[j, b][:],
                lhsT=d_codes[:, g, tokens].bitcast(FP8X4),
                lhsT_scale=d_scales[:, g, tokens],
                rhs=w_codes[:, g, columns].bitcast(FP8X4),
                rhs_scale=w_scales[:, g, columns],
                start=(g == 0),
                stop=(g == GROUPS - 1),
            )

        def second_matmul(j, b):
            second_bank(psum_side, "side", j, b)
            for g in range(GROUPS):
                second_pass(j, b, g)

        def empty(copy, j, b):
            i, h = divmod(b, HALVES)
            if h == 0:
                result = results.tile([P, CENTRES], F32)
                result_of[j, i] = result
            half = slice(h * BANK, (h + 1) * BANK)
            copy(out=result_of[j, i][:, half], in_=bank_of[j, b][:])
            if j == LAST:
                nc.sync.dma_start(out=chunk_rows(out, j)[:, i, half], in_=result_of[j, i][:, half])
            elif h == HALVES - 1:
                nc.sync.dma_start(out=chunk_rows(out, j)[:, i, :], in_=result_of[j, i][:])

        with tc.manual_schedule():
            token_squares(0, range(TILES), squares_by_scalar)
            new_token_words(0)
            for i in range(2):
                flipped = psum_xc.tile([P, 2, P], F32, tag="xc")
                transpose_tiles(nc, flipped, identity[:], token_rows(0)[:, i : i + 1, :])
                regroup(by_vector, flipped[:], token_words[0][:, i * P : (i + 1) * P, :])
            second_pair = transpose_pair(token_rows(0), 1)
            token_quantise(0, columns_of(0))
            regroup(by_vector, second_pair[:], token_words[0][:, columns_of(1), :])
            token_quantise(0, columns_of(1))
            centre_codes(0, centre_regroup(0, by_vector))
            centre_squares(0)
            spread_squares(0)
            centre_words = centre_regroup(1, by_scalar)
            keep_squares(0)
            centre_squares(1)
            for t in range(PACK):
                first_matmul(0, t)
            token_transposes(1)
            read_gamma()

            for u in range(drain):
                j, g, start, width = units[u]
                if u > 0 and u in REGROUPED_IN:
                    token_transposes(REGROUPED_IN[u])
                if g == 1:
                    spread_squares(j + 1)
                for t in reading_order(u):
                    distance(u, t)
                    if u > 0:
                        first_matmul(u + 1, t)
                exponential(u)
                if u + 1 < drain:
                    for strip in strips(u):
                        bound(nc.gpsimd, u, strip)
                if u in REGROUPED_IN:
                    token_regroup(REGROUPED_IN[u], 0)
                elif g == 1:
                    keep_squares(j + 1)
                if u > 0:
                    quantise(u - 1, whole(u - 1))
                if u in REGROUPED_IN:
                    token_regroup(REGROUPED_IN[u], 1)
                    if g == 1:
                        keep_squares(j + 1)
                if g == 1 and u in VECTOR_SQUARES_IN:
                    token_squares(LAST, [VECTOR_SQUARES_IN[u]], squares_by_vector)
                if u == 0:
                    centre_codes(1, centre_words)
                    for t in range(PACK):
                        first_matmul(1, t)
                    token_quantise(1, slice(0, CHUNK))
                    token_squares(1, range(TILES), squares_by_scalar)
                elif g == 0:
                    token_quantise(j + 1, slice(0, CHUNK))
                    if u in VECTOR_SQUARES_IN:
                        token_squares(LAST, [VECTOR_SQUARES_IN[u]], squares_by_vector)
                    for b in BANKS[:SIDE_BANKS]:
                        second_matmul(j - 1, b)
                    for b in BANKS[:SIDE_BANKS]:
                        empty(by_scalar, j - 1, b)
                else:
                    if j > 0:
                        for b in BANKS[SIDE_BANKS:]:
                            second_matmul(j - 1, b)
                        for b in BANKS[SIDE_BANKS:]:
                            empty(by_vector if b == VECTOR_BANK else by_scalar, j - 1, b)
                    if j + 2 <= LAST:
                        by_others = len(VECTOR_SQUARES_IN) if j + 2 == LAST else 0
                        token_squares(j + 2, range(TILES - by_others), squares_by_scalar)

            left = [(j, b) for j in (LAST - 1, LAST) for b in BANKS]
            ready = len(left) - 4
            issued = 0
            emptied = 0
            for u in range(drain, len(units)):
                for t in reading_order(u):
                    distance(u, t)
                    if u < final:
                        first_matmul(u + 1, t)
                exponential(u)
                for strip in strips(u - 1):
                    bound(nc.vector, u - 1, strip)
                if u > drain:
                    empty(by_vector, *left[emptied])
                    emptied += 1
                quantise(u - 1, whole(u - 1))
                upto = min(issued + (SIDE_BANKS if u == drain else 3), ready)
                for j, b in left[issued:upto]:
                    second_matmul(j, b)
                issued = upto
                for j, b in left[emptied : emptied + 2]:
                    empty(by_scalar, j, b)
                emptied += 2
            for j, b in left[ready:]:
                second_bank(psum_xc, "xc", j, b)
                second_pass(j, b, 0)
            for n, strip in enumerate(strips(final)):
                bound(nc.vector, final, strip)
                quantise(final, strip)
                for j, b in left[ready + HALVES * n : ready + HALVES * (n + 1)]:
                    second_pass(j, b, 1)
            for n, (j, b) in enumerate(left[emptied:]):
                empty(by_vector if n % 2 == 0 else by_scalar, j, b)
